import numpy as np
import ml_dtypes

BF16 = ml_dtypes.bfloat16


def bf(x):
    return np.asarray(x, np.float32).astype(BF16)


def f32(x):
    return np.asarray(x, np.float32)


def f64(x):
    return np.asarray(x).astype(np.float64)


def striped(idx):
    return np.tile(idx.reshape(-1, 16).T, (8, 1))


C, S, K, N, H = 256, 2048, 4, 8192, 1024
ALPHA = 0.3


def setup_inputs():
    return {"x": f32(np.random.standard_normal((C, S))), "p_dst": f32(np.random.standard_normal((C, 1)) / np.sqrt(C)), "p_src": f32(np.random.standard_normal((C, 1)) / np.sqrt(C)), "offs": striped(np.concatenate([np.random.permutation(S)[:H] for _ in range(N // H)]))}


def reference(x, p_dst, p_src, offs):
    idx = offs[:16].T.reshape(-1)
    x = f64(x)
    xg = x[:, idx]
    v = (f64(p_src) * xg).sum(axis=0) + np.repeat((f64(p_dst) * x).sum(axis=0), K)
    e = np.maximum(v, ALPHA * v)
    ep = np.exp(e).reshape(S, K)
    en = np.exp(-e).reshape(S, K)
    a_pos = (ep / ep.sum(axis=1, keepdims=True)).reshape(N)
    a_neg = (-en / en.sum(axis=1, keepdims=True)).reshape(N)
    pos = (xg * a_pos).reshape(C, S, K).sum(axis=2)
    neg = (xg * a_neg).reshape(C, S, K).sum(axis=2)
    return np.concatenate([pos, neg], axis=0)

@@ -1,0 +1,167 @@
+from contextlib import ExitStack
+
+import concourse.mybir as mybir
+from concourse.masks import make_identity
+
+F32 = mybir.dt.float32
+BF16 = mybir.dt.bfloat16
+U16 = mybir.dt.uint16
+ALU = mybir.AluOpType
+ACT = mybir.ActivationFunctionType
+AXIS = mybir.AxisListType
+
+P = 128
+C, S, K, N = 256, 2048, 4, 8192
+BLOCKS = C // P
+SLOPE = 0.3
+PIECE = 2048
+PIECES = N // PIECE
+NODES = PIECE // K
+PER = PIECE // P
+NQ = PER // K
+LEAD = 2
+CLAMP = 80.0
+SIGNS = 2
+PARK_ROWS = PIECE // NODES
+PARK_ROW0 = SIGNS * C - SIGNS * PARK_ROWS
+
+FLOPS = 2 * C * N + 2 * C * S + SIGNS * 2 * C * N
+
+
+def tile_signed_gat_kernel(tc, x, p_dst, p_src, offs, out):
+    nc = tc.nc
+    with ExitStack() as ctx:
+        held = ctx.enter_context(tc.tile_pool(name="held", bufs=1))
+        prod_pool = ctx.enter_context(tc.tile_pool(name="prod", bufs=2))
+        small = ctx.enter_context(tc.tile_pool(name="small", bufs=2))
+        weight_pool = ctx.enter_context(tc.tile_pool(name="weights", bufs=PIECES))
+        picked_pool = ctx.enter_context(tc.tile_pool(name="picked", bufs=3))
+        result_pool = ctx.enter_context(tc.tile_pool(name="result", bufs=3))
+        psum_v = ctx.enter_context(tc.psum_pool(name="psum_v", bufs=2))
+        psum_sum = ctx.enter_context(tc.psum_pool(name="psum_sum", bufs=4))
+
+        offsets = held.tile([P, N // 16], U16, name="offsets")
+        nc.sync.dma_start(offsets[:], offs)
+        src_w = held.tile([P, BLOCKS], F32, name="src_w")
+        dst_w = held.tile([P, BLOCKS], F32, name="dst_w")
+        with nc.allow_non_contiguous_dma(reason="256 floats, one to a partition and block"):
+            nc.scalar.dma_start(src_w[:], p_src.rearrange("(b c) o -> c (b o)", b=BLOCKS))
+            nc.scalar.dma_start(dst_w[:], p_dst.rearrange("(b c) o -> c (b o)", b=BLOCKS))
+        table = [held.tile([P, S], F32, name=f"table{b}") for b in range(BLOCKS)]
+        nc.sync.dma_start(table[0][:], x[0:P, :])
+        nc.scalar.dma_start(table[1][:], x[P : 2 * P, :])
+
+        identity = held.tile([P, P], F32, name="identity")
+        make_identity(nc, identity[:])
+        one_hot = held.tile([P, K, K], BF16, name="one_hot")
+        nc.gpsimd.memset(one_hot[:], 0.0)
+        for t in range(K):
+            nc.gpsimd.memset(one_hot[:, t, t : t + 1], 1.0)
+        src_wide = [held.tile([P, PIECE], F32, name=f"src_wide{b}") for b in range(BLOCKS)]
+        for b in range(BLOCKS):
+            nc.vector.tensor_copy(src_wide[b][:], src_w[:, b : b + 1].to_broadcast([P, PIECE]))
+        dst_w4 = held.tile([P, BLOCKS, K], F32, name="dst_w4")
+        nc.vector.tensor_copy(dst_w4[:], dst_w[:].unsqueeze(2).to_broadcast([P, BLOCKS, K]))
+
+        def piece_offsets(k):
+            return offsets[:, k * (PIECE // 16) : (k + 1) * (PIECE // 16)]
+
+        def attention_weights(k):
+            products = []
+            for b in range(BLOCKS):
+                prod = prod_pool.tile([P, PIECE], F32, name="prod")
+                nc.vector.tensor_tensor(
+                    prod[:],
+                    table[b][:].indirect(piece_offsets(k)),
+                    src_wide[b][:],
+                    ALU.mult,
+                )
+                prod_bf = prod_pool.tile([P, PIECE], BF16, name=f"prod_bf{b}")
+                nc.scalar.activation(prod_bf[:], prod[:], ACT.Copy)
+                products.append(prod_bf)
+
+            v = psum_v.tile([P, NQ, K], F32, name="v")
+            for q in range(NQ):
+                for b in range(BLOCKS):
+                    own = table[b][:, k * NODES : (k + 1) * NODES].rearrange("c (p q) -> c q p", q=NQ)
+                    nc.tensor.matmul(
+                        v[:, q, :], lhsT=own[:, q, :], rhs=dst_w4[:, b, :], start=(b == 0), stop=False
+                    )
+                for t in range(K):
+                    for b in range(BLOCKS):
+                        by_entry = products[b][:].rearrange("c (p f) -> c f p", f=PER)
+                        nc.tensor.matmul(
+                            v[:, q, :],
+                            lhsT=by_entry[:, q * K + t, :],
+                            rhs=one_hot[:, t, :],
+                            start=False,
+                            stop=(t == K - 1 and b == BLOCKS - 1),
+                        )
+
+            sloped = small.tile([P, NQ, K], F32, name="sloped")
+            nc.vector.tensor_scalar_mul(sloped[:], v[:], SLOPE)
+            e = small.tile([P, NQ, K], F32, name="e")
+            nc.vector.tensor_tensor(e[:], sloped[:], v[:], ALU.max)
+            diff = small.tile([P, NQ, K, K], F32, name="diff")
+            nc.vector.tensor_tensor(
+                diff[:],
+                e[:].unsqueeze(2).to_broadcast([P, NQ, K, K]),
+                e[:].unsqueeze(3).to_broadcast([P, NQ, K, K]),
+                ALU.subtract,
+            )
+            nc.vector.tensor_scalar(diff[:], diff[:], CLAMP, -CLAMP, ALU.min, ALU.max)
+            terms = small.tile([P, SIGNS, NQ, K, K], F32, name="terms")
+            nc.scalar.activation(terms[:, 0], diff[:], ACT.Exp)
+            nc.scalar.activation(terms[:, 1], diff[:], ACT.Exp, scale=-1.0)
+            denom = small.tile([P, SIGNS, NQ, K], F32, name="denom")
+            nc.vector.tensor_reduce(denom[:, 0], terms[:, 0], axis=AXIS.X, op=ALU.add)
+            nc.vector.tensor_reduce(denom[:, 1], terms[:, 1], axis=AXIS.X, op=ALU.add, negate=True)
+            att = small.tile([P, SIGNS, NQ, K], F32, name="att")
+            nc.vector.reciprocal(att[:], denom[:])
+
+            park = out[PARK_ROW0 : PARK_ROW0 + SIGNS * PARK_ROWS, k * NODES : (k + 1) * NODES]
+            park_by_row = park.rearrange("(s h) (l f) -> h l s f", s=SIGNS, f=PER)
+            lanes = P // PARK_ROWS
+            for h in range(PARK_ROWS):
+                nc.sync.dma_start(
+                    park_by_row[h],
+                    att[h * lanes : (h + 1) * lanes].rearrange("l s q t -> l s (q t)"),
+                )
+            weights = weight_pool.tile([P, SIGNS, PIECE], F32, name="weights")
+            for s in range(SIGNS):
+                nc.sync.dma_start(
+                    weights[:, s, :].rearrange("c (h w) -> c h w", w=NODES),
+                    park[s * PARK_ROWS : (s + 1) * PARK_ROWS, :]
+                    .unsqueeze(0)
+                    .to_broadcast([P, PARK_ROWS, NODES]),
+                )
+            return weights
+
+        def weighted_sums(k, weights):
+            for s in range(SIGNS):
+                for b in range(BLOCKS):
+                    picked = picked_pool.tile([P, PIECE], F32, name="picked")
+                    nc.vector.tensor_tensor(
+                        picked[:], table[b][:].indirect(piece_offsets(k)), weights[:, s, :], ALU.mult
+                    )
+                    by_neighbour = picked[:].rearrange("c (i t) -> c t i", t=K)
+                    total = psum_sum.tile([P, NODES], F32, name="total")
+                    for t in range(K):
+                        nc.tensor.matmul(
+                            total[:],
+                            lhsT=identity[:],
+                            rhs=by_neighbour[:, t, :],
+                            start=(t == 0),
+                            stop=(t == K - 1),
+                        )
+                    result = result_pool.tile([P, NODES], F32, name="result")
+                    nc.scalar.activation(result[:], total[:], ACT.Copy)
+                    row0 = (s * BLOCKS + b) * P
+                    nc.scalar.dma_start(out[row0 : row0 + P, k * NODES : (k + 1) * NODES], result[:])
+
+        ready = []
+        for step in range(PIECES + LEAD):
+            if step < PIECES:
+                ready.append(attention_weights(step))
+            if step >= LEAD:
+                weighted_sums(step - LEAD, ready[step - LEAD])

@@ -36,6 +36,7 @@ def tile_signed_gat_kernel(tc, x, p_dst, p_src, offs, out):
         small = ctx.enter_context(tc.tile_pool(name="small", bufs=2))
         weight_pool = ctx.enter_context(tc.tile_pool(name="weights", bufs=PIECES))
         picked_pool = ctx.enter_context(tc.tile_pool(name="picked", bufs=3))
+        plane_pool = ctx.enter_context(tc.tile_pool(name="planes", bufs=3))
         result_pool = ctx.enter_context(tc.tile_pool(name="result", bufs=3))
         psum_v = ctx.enter_context(tc.psum_pool(name="psum_v", bufs=2))
         psum_sum = ctx.enter_context(tc.psum_pool(name="psum_sum", bufs=4))
@@ -144,13 +145,18 @@ def tile_signed_gat_kernel(tc, x, p_dst, p_src, offs, out):
                     nc.vector.tensor_tensor(
                         picked[:], table[b][:].indirect(piece_offsets(k)), weights[:, s, :], ALU.mult
                     )
-                    by_neighbour = picked[:].rearrange("c (i t) -> c t i", t=K)
+                    planes = plane_pool.tile([P, K, NODES], F32, name="planes")
+                    nc.scalar.activation(
+                        planes[:].rearrange("c t i -> c i t"),
+                        picked[:].rearrange("c (i t) -> c i t", t=K),
+                        ACT.Copy,
+                    )
                     total = psum_sum.tile([P, NODES], F32, name="total")
                     for t in range(K):
                         nc.tensor.matmul(
                             total[:],
                             lhsT=identity[:],
-                            rhs=by_neighbour[:, t, :],
+                            rhs=planes[:, t, :],
                             start=(t == 0),
                             stop=(t == K - 1),
                         )

@@ -19,7 +19,6 @@ PIECES = N // PIECE
 NODES = PIECE // K
 PER = PIECE // P
 NQ = PER // K
-LEAD = 2
 CLAMP = 80.0
 SIGNS = 2
 PARK_ROWS = PIECE // NODES
@@ -33,12 +32,13 @@ def tile_signed_gat_kernel(tc, x, p_dst, p_src, offs, out):
     with ExitStack() as ctx:
         held = ctx.enter_context(tc.tile_pool(name="held", bufs=1))
         prod_pool = ctx.enter_context(tc.tile_pool(name="prod", bufs=2))
+        round_pool = ctx.enter_context(tc.tile_pool(name="rounded", bufs=1))
         small = ctx.enter_context(tc.tile_pool(name="small", bufs=2))
         weight_pool = ctx.enter_context(tc.tile_pool(name="weights", bufs=PIECES))
         picked_pool = ctx.enter_context(tc.tile_pool(name="picked", bufs=3))
         plane_pool = ctx.enter_context(tc.tile_pool(name="planes", bufs=3))
         result_pool = ctx.enter_context(tc.tile_pool(name="result", bufs=3))
-        psum_v = ctx.enter_context(tc.psum_pool(name="psum_v", bufs=2))
+        psum_v = ctx.enter_context(tc.psum_pool(name="psum_v", bufs=PIECES))
         psum_sum = ctx.enter_context(tc.psum_pool(name="psum_sum", bufs=4))
 
         offsets = held.tile([P, N // 16], U16, name="offsets")
@@ -49,20 +49,24 @@ def tile_signed_gat_kernel(tc, x, p_dst, p_src, offs, out):
             nc.scalar.dma_start(src_w[:], p_src.rearrange("(b c) o -> c (b o)", b=BLOCKS))
             nc.scalar.dma_start(dst_w[:], p_dst.rearrange("(b c) o -> c (b o)", b=BLOCKS))
         table = [held.tile([P, S], F32, name=f"table{b}") for b in range(BLOCKS)]
-        nc.sync.dma_start(table[0][:], x[0:P, :])
-        nc.scalar.dma_start(table[1][:], x[P : 2 * P, :])
+        for b in range(BLOCKS):
+            nc.sync.dma_start(table[b][:], x[b * P : (b + 1) * P, :])
 
         identity = held.tile([P, P], F32, name="identity")
         make_identity(nc, identity[:])
-        one_hot = held.tile([P, K, K], BF16, name="one_hot")
+        one_hot = held.tile([P, PER, PER], BF16, name="one_hot")
         nc.gpsimd.memset(one_hot[:], 0.0)
-        for t in range(K):
-            nc.gpsimd.memset(one_hot[:, t, t : t + 1], 1.0)
+        for f in range(PER):
+            nc.gpsimd.memset(one_hot[:, f, f : f + 1], 1.0)
         src_wide = [held.tile([P, PIECE], F32, name=f"src_wide{b}") for b in range(BLOCKS)]
-        for b in range(BLOCKS):
-            nc.vector.tensor_copy(src_wide[b][:], src_w[:, b : b + 1].to_broadcast([P, PIECE]))
-        dst_w4 = held.tile([P, BLOCKS, K], F32, name="dst_w4")
-        nc.vector.tensor_copy(dst_w4[:], dst_w[:].unsqueeze(2).to_broadcast([P, BLOCKS, K]))
+        nc.vector.tensor_copy(src_wide[0][:], src_w[:, 0:1].to_broadcast([P, PIECE]))
+        nc.scalar.activation(src_wide[1][:], src_w[:, 1:2].to_broadcast([P, PIECE]), ACT.Copy)
+        dst_cols = held.tile([P, BLOCKS, NQ, PER], F32, name="dst_cols")
+        nc.gpsimd.memset(dst_cols[:], 0.0)
+        for q in range(NQ):
+            nc.gpsimd.tensor_copy(
+                dst_cols[:, :, q, q * K : (q + 1) * K], dst_w[:].unsqueeze(2).to_broadcast([P, BLOCKS, K])
+            )
 
         def piece_offsets(k):
             return offsets[:, k * (PIECE // 16) : (k + 1) * (PIECE // 16)]
@@ -77,27 +81,28 @@ def tile_signed_gat_kernel(tc, x, p_dst, p_src, offs, out):
                     src_wide[b][:],
                     ALU.mult,
                 )
-                prod_bf = prod_pool.tile([P, PIECE], BF16, name=f"prod_bf{b}")
+                prod_bf = round_pool.tile([P, PIECE], BF16, name=f"prod_bf{b}")
                 nc.scalar.activation(prod_bf[:], prod[:], ACT.Copy)
                 products.append(prod_bf)
 
             v = psum_v.tile([P, NQ, K], F32, name="v")
-            for q in range(NQ):
-                for b in range(BLOCKS):
-                    own = table[b][:, k * NODES : (k + 1) * NODES].rearrange("c (p q) -> c q p", q=NQ)
+            v_flat = v[:].rearrange("p q t -> p (q t)")
+            for b in range(BLOCKS):
+                own = table[b][:, k * NODES : (k + 1) * NODES].rearrange("c (p q) -> c q p", q=NQ)
+                for q in range(NQ):
                     nc.tensor.matmul(
-                        v[:, q, :], lhsT=own[:, q, :], rhs=dst_w4[:, b, :], start=(b == 0), stop=False
+                        v_flat, lhsT=own[:, q, :], rhs=dst_cols[:, b, q, :], start=(b == 0 and q == 0), stop=False
                     )
-                for t in range(K):
-                    for b in range(BLOCKS):
-                        by_entry = products[b][:].rearrange("c (p f) -> c f p", f=PER)
-                        nc.tensor.matmul(
-                            v[:, q, :],
-                            lhsT=by_entry[:, q * K + t, :],
-                            rhs=one_hot[:, t, :],
-                            start=False,
-                            stop=(t == K - 1 and b == BLOCKS - 1),
-                        )
+            for b in range(BLOCKS):
+                by_entry = products[b][:].rearrange("c (p f) -> c f p", f=PER)
+                for f in range(PER):
+                    nc.tensor.matmul(
+                        v_flat,
+                        lhsT=by_entry[:, f, :],
+                        rhs=one_hot[:, f, :],
+                        start=False,
+                        stop=(b == BLOCKS - 1 and f == PER - 1),
+                    )
 
             sloped = small.tile([P, NQ, K], F32, name="sloped")
             nc.vector.tensor_scalar_mul(sloped[:], v[:], SLOPE)
@@ -145,6 +150,14 @@ def tile_signed_gat_kernel(tc, x, p_dst, p_src, offs, out):
                     nc.vector.tensor_tensor(
                         picked[:], table[b][:].indirect(piece_offsets(k)), weights[:, s, :], ALU.mult
                     )
+                    result = result_pool.tile([P, NODES], F32, name="result")
+                    row0 = (s * BLOCKS + b) * P
+                    if k == PIECES - 1 and s == SIGNS - 1 and b == BLOCKS - 1:
+                        nc.vector.tensor_reduce(
+                            result[:], picked[:].rearrange("c (i t) -> c i t", t=K), axis=AXIS.X, op=ALU.add
+                        )
+                        nc.sync.dma_start(out[row0 : row0 + P, k * NODES : (k + 1) * NODES], result[:])
+                        continue
                     planes = plane_pool.tile([P, K, NODES], F32, name="planes")
                     nc.scalar.activation(
                         planes[:].rearrange("c t i -> c i t"),
@@ -160,14 +173,9 @@ def tile_signed_gat_kernel(tc, x, p_dst, p_src, offs, out):
                             start=(t == 0),
                             stop=(t == K - 1),
                         )
-                    result = result_pool.tile([P, NODES], F32, name="result")
                     nc.scalar.activation(result[:], total[:], ACT.Copy)
-                    row0 = (s * BLOCKS + b) * P
                     nc.scalar.dma_start(out[row0 : row0 + P, k * NODES : (k + 1) * NODES], result[:])
 
-        ready = []
-        for step in range(PIECES + LEAD):
-            if step < PIECES:
-                ready.append(attention_weights(step))
-            if step >= LEAD:
-                weighted_sums(step - LEAD, ready[step - LEAD])
+        weights = [attention_weights(k) for k in range(PIECES)]
+        for k in range(PIECES):
+            weighted_sums(k, weights[k])

@@ -32,13 +32,12 @@ def tile_signed_gat_kernel(tc, x, p_dst, p_src, offs, out):
     with ExitStack() as ctx:
         held = ctx.enter_context(tc.tile_pool(name="held", bufs=1))
         prod_pool = ctx.enter_context(tc.tile_pool(name="prod", bufs=2))
-        round_pool = ctx.enter_context(tc.tile_pool(name="rounded", bufs=1))
         small = ctx.enter_context(tc.tile_pool(name="small", bufs=2))
         weight_pool = ctx.enter_context(tc.tile_pool(name="weights", bufs=PIECES))
         picked_pool = ctx.enter_context(tc.tile_pool(name="picked", bufs=3))
         plane_pool = ctx.enter_context(tc.tile_pool(name="planes", bufs=3))
         result_pool = ctx.enter_context(tc.tile_pool(name="result", bufs=3))
-        psum_v = ctx.enter_context(tc.psum_pool(name="psum_v", bufs=PIECES))
+        psum_v = ctx.enter_context(tc.psum_pool(name="psum_v", bufs=2))
         psum_sum = ctx.enter_context(tc.psum_pool(name="psum_sum", bufs=4))
 
         offsets = held.tile([P, N // 16], U16, name="offsets")
@@ -49,8 +48,8 @@ def tile_signed_gat_kernel(tc, x, p_dst, p_src, offs, out):
             nc.scalar.dma_start(src_w[:], p_src.rearrange("(b c) o -> c (b o)", b=BLOCKS))
             nc.scalar.dma_start(dst_w[:], p_dst.rearrange("(b c) o -> c (b o)", b=BLOCKS))
         table = [held.tile([P, S], F32, name=f"table{b}") for b in range(BLOCKS)]
-        for b in range(BLOCKS):
-            nc.sync.dma_start(table[b][:], x[b * P : (b + 1) * P, :])
+        nc.sync.dma_start(table[0][:], x[0:P, :])
+        nc.scalar.dma_start(table[1][:], x[P : 2 * P, :])
 
         identity = held.tile([P, P], F32, name="identity")
         make_identity(nc, identity[:])
@@ -59,13 +58,18 @@ def tile_signed_gat_kernel(tc, x, p_dst, p_src, offs, out):
         for f in range(PER):
             nc.gpsimd.memset(one_hot[:, f, f : f + 1], 1.0)
         src_wide = [held.tile([P, PIECE], F32, name=f"src_wide{b}") for b in range(BLOCKS)]
-        nc.vector.tensor_copy(src_wide[0][:], src_w[:, 0:1].to_broadcast([P, PIECE]))
-        nc.scalar.activation(src_wide[1][:], src_w[:, 1:2].to_broadcast([P, PIECE]), ACT.Copy)
-        dst_cols = held.tile([P, BLOCKS, NQ, PER], F32, name="dst_cols")
+        for b in range(BLOCKS):
+            nc.vector.tensor_copy(src_wide[b][:], src_w[:, b : b + 1].to_broadcast([P, PIECE]))
+        dst_cols = held.tile([P, BLOCKS, NQ, PER], BF16, name="dst_cols")
         nc.gpsimd.memset(dst_cols[:], 0.0)
         for q in range(NQ):
             nc.gpsimd.tensor_copy(
                 dst_cols[:, :, q, q * K : (q + 1) * K], dst_w[:].unsqueeze(2).to_broadcast([P, BLOCKS, K])
+            )
+        own = [held.tile([P, NQ, S // NQ], BF16, name=f"own{b}") for b in range(BLOCKS)]
+        for b in range(BLOCKS):
+            nc.scalar.activation(
+                own[b][:].rearrange("c q n -> c n q"), table[b][:].rearrange("c (n q) -> c n q", q=NQ), ACT.Copy
             )
 
         def piece_offsets(k):
@@ -81,24 +85,31 @@ def tile_signed_gat_kernel(tc, x, p_dst, p_src, offs, out):
                     src_wide[b][:],
                     ALU.mult,
                 )
-                prod_bf = round_pool.tile([P, PIECE], BF16, name=f"prod_bf{b}")
-                nc.scalar.activation(prod_bf[:], prod[:], ACT.Copy)
+                prod_bf = prod_pool.tile([P, PER, P], BF16, name=f"prod_bf{b}")
+                for q in range(NQ):
+                    nc.scalar.activation(
+                        prod_bf[:, q * K : (q + 1) * K, :].rearrange("c t p -> c p t"),
+                        prod[:].rearrange("c (p f) -> c p f", f=PER)[:, :, q * K : (q + 1) * K],
+                        ACT.Copy,
+                    )
                 products.append(prod_bf)
 
             v = psum_v.tile([P, NQ, K], F32, name="v")
             v_flat = v[:].rearrange("p q t -> p (q t)")
             for b in range(BLOCKS):
-                own = table[b][:, k * NODES : (k + 1) * NODES].rearrange("c (p q) -> c q p", q=NQ)
                 for q in range(NQ):
                     nc.tensor.matmul(
-                        v_flat, lhsT=own[:, q, :], rhs=dst_cols[:, b, q, :], start=(b == 0 and q == 0), stop=False
+                        v_flat,
+                        lhsT=own[b][:, q, k * P : (k + 1) * P],
+                        rhs=dst_cols[:, b, q, :],
+                        start=(b == 0 and q == 0),
+                        stop=False,
                     )
             for b in range(BLOCKS):
-                by_entry = products[b][:].rearrange("c (p f) -> c f p", f=PER)
                 for f in range(PER):
                     nc.tensor.matmul(
                         v_flat,
-                        lhsT=by_entry[:, f, :],
+                        lhsT=products[b][:, f, :],
                         rhs=one_hot[:, f, :],
                         start=False,
                         stop=(b == BLOCKS - 1 and f == PER - 1),

@@ -19,7 +19,6 @@ PIECES = N // PIECE
 NODES = PIECE // K
 PER = PIECE // P
 NQ = PER // K
-CLAMP = 80.0
 SIGNS = 2
 PARK_ROWS = PIECE // NODES
 PARK_ROW0 = SIGNS * C - SIGNS * PARK_ROWS
@@ -116,23 +115,32 @@ def tile_signed_gat_kernel(tc, x, p_dst, p_src, offs, out):
                     )
 
             sloped = small.tile([P, NQ, K], F32, name="sloped")
-            nc.vector.tensor_scalar_mul(sloped[:], v[:], SLOPE)
+            nc.scalar.activation(sloped[:], v[:], ACT.Copy, scale=SLOPE)
             e = small.tile([P, NQ, K], F32, name="e")
             nc.vector.tensor_tensor(e[:], sloped[:], v[:], ALU.max)
-            diff = small.tile([P, NQ, K, K], F32, name="diff")
-            nc.vector.tensor_tensor(
-                diff[:],
-                e[:].unsqueeze(2).to_broadcast([P, NQ, K, K]),
-                e[:].unsqueeze(3).to_broadcast([P, NQ, K, K]),
-                ALU.subtract,
-            )
-            nc.vector.tensor_scalar(diff[:], diff[:], CLAMP, -CLAMP, ALU.min, ALU.max)
-            terms = small.tile([P, SIGNS, NQ, K, K], F32, name="terms")
-            nc.scalar.activation(terms[:, 0], diff[:], ACT.Exp)
-            nc.scalar.activation(terms[:, 1], diff[:], ACT.Exp, scale=-1.0)
+            minus_e = small.tile([P, NQ, K], F32, name="minus_e")
+            nc.scalar.activation(minus_e[:], e[:], ACT.Copy, scale=-1.0)
             denom = small.tile([P, SIGNS, NQ, K], F32, name="denom")
-            nc.vector.tensor_reduce(denom[:, 0], terms[:, 0], axis=AXIS.X, op=ALU.add)
-            nc.vector.tensor_reduce(denom[:, 1], terms[:, 1], axis=AXIS.X, op=ALU.add, negate=True)
+            terms = small.tile([P, SIGNS, NQ, K, K], F32, name="terms")
+            for q in range(NQ):
+                for t in range(K):
+                    nc.scalar.activation(
+                        terms[:, 0, q, t, :],
+                        e[:, q, :],
+                        ACT.Exp,
+                        bias=minus_e[:, q, t : t + 1],
+                        scale=1.0,
+                        accum_out=denom[:, 0, q, t : t + 1],
+                    )
+                    nc.scalar.activation(
+                        terms[:, 1, q, t, :],
+                        e[:, q, :],
+                        ACT.Exp,
+                        bias=e[:, q, t : t + 1],
+                        scale=-1.0,
+                        accum_out=denom[:, 1, q, t : t + 1],
+                    )
+            nc.scalar.activation(denom[:, 1], denom[:, 1], ACT.Copy, scale=-1.0)
             att = small.tile([P, SIGNS, NQ, K], F32, name="att")
             nc.vector.reciprocal(att[:], denom[:])
 

@@ -47,8 +47,8 @@ def tile_signed_gat_kernel(tc, x, p_dst, p_src, offs, out):
             nc.scalar.dma_start(src_w[:], p_src.rearrange("(b c) o -> c (b o)", b=BLOCKS))
             nc.scalar.dma_start(dst_w[:], p_dst.rearrange("(b c) o -> c (b o)", b=BLOCKS))
         table = [held.tile([P, S], F32, name=f"table{b}") for b in range(BLOCKS)]
-        nc.sync.dma_start(table[0][:], x[0:P, :])
-        nc.scalar.dma_start(table[1][:], x[P : 2 * P, :])
+        for b in range(BLOCKS):
+            nc.sync.dma_start(table[b][:], x[b * P : (b + 1) * P, :])
 
         identity = held.tile([P, P], F32, name="identity")
         make_identity(nc, identity[:])
@@ -57,8 +57,8 @@ def tile_signed_gat_kernel(tc, x, p_dst, p_src, offs, out):
         for f in range(PER):
             nc.gpsimd.memset(one_hot[:, f, f : f + 1], 1.0)
         src_wide = [held.tile([P, PIECE], F32, name=f"src_wide{b}") for b in range(BLOCKS)]
-        for b in range(BLOCKS):
-            nc.vector.tensor_copy(src_wide[b][:], src_w[:, b : b + 1].to_broadcast([P, PIECE]))
+        nc.vector.tensor_copy(src_wide[0][:], src_w[:, 0:1].to_broadcast([P, PIECE]))
+        nc.scalar.activation(src_wide[1][:], src_w[:, 1:2].to_broadcast([P, PIECE]), ACT.Copy)
         dst_cols = held.tile([P, BLOCKS, NQ, PER], BF16, name="dst_cols")
         nc.gpsimd.memset(dst_cols[:], 0.0)
         for q in range(NQ):

@@ -30,7 +30,7 @@ def tile_signed_gat_kernel(tc, x, p_dst, p_src, offs, out):
     nc = tc.nc
     with ExitStack() as ctx:
         held = ctx.enter_context(tc.tile_pool(name="held", bufs=1))
-        prod_pool = ctx.enter_context(tc.tile_pool(name="prod", bufs=2))
+        prod_pool = ctx.enter_context(tc.tile_pool(name="prod", bufs=3))
         small = ctx.enter_context(tc.tile_pool(name="small", bufs=2))
         weight_pool = ctx.enter_context(tc.tile_pool(name="weights", bufs=PIECES))
         picked_pool = ctx.enter_context(tc.tile_pool(name="picked", bufs=3))
@@ -47,8 +47,8 @@ def tile_signed_gat_kernel(tc, x, p_dst, p_src, offs, out):
             nc.scalar.dma_start(src_w[:], p_src.rearrange("(b c) o -> c (b o)", b=BLOCKS))
             nc.scalar.dma_start(dst_w[:], p_dst.rearrange("(b c) o -> c (b o)", b=BLOCKS))
         table = [held.tile([P, S], F32, name=f"table{b}") for b in range(BLOCKS)]
-        for b in range(BLOCKS):
-            nc.sync.dma_start(table[b][:], x[b * P : (b + 1) * P, :])
+        nc.sync.dma_start(table[0][:], x[0:P, :])
+        nc.scalar.dma_start(table[1][:], x[P : 2 * P, :])
 
         identity = held.tile([P, P], F32, name="identity")
         make_identity(nc, identity[:])
@@ -57,8 +57,8 @@ def tile_signed_gat_kernel(tc, x, p_dst, p_src, offs, out):
         for f in range(PER):
             nc.gpsimd.memset(one_hot[:, f, f : f + 1], 1.0)
         src_wide = [held.tile([P, PIECE], F32, name=f"src_wide{b}") for b in range(BLOCKS)]
-        nc.vector.tensor_copy(src_wide[0][:], src_w[:, 0:1].to_broadcast([P, PIECE]))
-        nc.scalar.activation(src_wide[1][:], src_w[:, 1:2].to_broadcast([P, PIECE]), ACT.Copy)
+        for b in range(BLOCKS):
+            nc.vector.tensor_copy(src_wide[b][:], src_w[:, b : b + 1].to_broadcast([P, PIECE]))
         dst_cols = held.tile([P, BLOCKS, NQ, PER], BF16, name="dst_cols")
         nc.gpsimd.memset(dst_cols[:], 0.0)
         for q in range(NQ):
@@ -121,26 +121,20 @@ def tile_signed_gat_kernel(tc, x, p_dst, p_src, offs, out):
             minus_e = small.tile([P, NQ, K], F32, name="minus_e")
             nc.scalar.activation(minus_e[:], e[:], ACT.Copy, scale=-1.0)
             denom = small.tile([P, SIGNS, NQ, K], F32, name="denom")
-            terms = small.tile([P, SIGNS, NQ, K, K], F32, name="terms")
+            terms = small.tile([P, NQ, K, K], F32, name="terms")
             for q in range(NQ):
                 for t in range(K):
                     nc.scalar.activation(
-                        terms[:, 0, q, t, :],
+                        terms[:, q, t, :],
                         e[:, q, :],
                         ACT.Exp,
                         bias=minus_e[:, q, t : t + 1],
                         scale=1.0,
                         accum_out=denom[:, 0, q, t : t + 1],
                     )
-                    nc.scalar.activation(
-                        terms[:, 1, q, t, :],
-                        e[:, q, :],
-                        ACT.Exp,
-                        bias=e[:, q, t : t + 1],
-                        scale=-1.0,
-                        accum_out=denom[:, 1, q, t : t + 1],
-                    )
-            nc.scalar.activation(denom[:, 1], denom[:, 1], ACT.Copy, scale=-1.0)
+            nc.vector.tensor_reduce(
+                denom[:, 1], terms[:].rearrange("p q t u -> p q u t"), axis=AXIS.X, op=ALU.add, negate=True
+            )
             att = small.tile([P, SIGNS, NQ, K], F32, name="att")
             nc.vector.reciprocal(att[:], denom[:])
 

@@ -30,13 +30,14 @@ def tile_signed_gat_kernel(tc, x, p_dst, p_src, offs, out):
     nc = tc.nc
     with ExitStack() as ctx:
         held = ctx.enter_context(tc.tile_pool(name="held", bufs=1))
-        prod_pool = ctx.enter_context(tc.tile_pool(name="prod", bufs=3))
+        prod_pool = ctx.enter_context(tc.tile_pool(name="prod", bufs=2))
         small = ctx.enter_context(tc.tile_pool(name="small", bufs=2))
         weight_pool = ctx.enter_context(tc.tile_pool(name="weights", bufs=PIECES))
         picked_pool = ctx.enter_context(tc.tile_pool(name="picked", bufs=3))
         plane_pool = ctx.enter_context(tc.tile_pool(name="planes", bufs=3))
         result_pool = ctx.enter_context(tc.tile_pool(name="result", bufs=3))
         psum_v = ctx.enter_context(tc.psum_pool(name="psum_v", bufs=2))
+        psum_e = ctx.enter_context(tc.psum_pool(name="psum_e", bufs=2))
         psum_sum = ctx.enter_context(tc.psum_pool(name="psum_sum", bufs=4))
 
         offsets = held.tile([P, N // 16], U16, name="offsets")
@@ -114,27 +115,43 @@ def tile_signed_gat_kernel(tc, x, p_dst, p_src, offs, out):
                         stop=(b == BLOCKS - 1 and f == PER - 1),
                     )
 
-            sloped = small.tile([P, NQ, K], F32, name="sloped")
-            nc.scalar.activation(sloped[:], v[:], ACT.Copy, scale=SLOPE)
+            parts = small.tile([P, 2, PER], F32, name="parts")
+            nc.scalar.activation(parts[:, 0, :], v_flat, ACT.Relu, scale=1.0 - SLOPE)
+            nc.scalar.activation(parts[:, 1, :], v_flat, ACT.Copy, scale=SLOPE)
+            e_sum = psum_e.tile([P, NQ, K], F32, name="e_sum")
+            for h in range(2):
+                nc.tensor.matmul(
+                    e_sum[:].rearrange("p q t -> p (q t)"),
+                    lhsT=identity[:],
+                    rhs=parts[:, h, :],
+                    start=(h == 0),
+                    stop=(h == 1),
+                )
             e = small.tile([P, NQ, K], F32, name="e")
-            nc.vector.tensor_tensor(e[:], sloped[:], v[:], ALU.max)
+            nc.scalar.activation(e[:], e_sum[:], ACT.Copy)
             minus_e = small.tile([P, NQ, K], F32, name="minus_e")
-            nc.scalar.activation(minus_e[:], e[:], ACT.Copy, scale=-1.0)
+            nc.scalar.activation(minus_e[:], e_sum[:], ACT.Copy, scale=-1.0)
             denom = small.tile([P, SIGNS, NQ, K], F32, name="denom")
-            terms = small.tile([P, NQ, K, K], F32, name="terms")
+            terms = small.tile([P, SIGNS, NQ, K, K], F32, name="terms")
             for q in range(NQ):
                 for t in range(K):
                     nc.scalar.activation(
-                        terms[:, q, t, :],
+                        terms[:, 0, q, t, :],
                         e[:, q, :],
                         ACT.Exp,
                         bias=minus_e[:, q, t : t + 1],
                         scale=1.0,
                         accum_out=denom[:, 0, q, t : t + 1],
                     )
-            nc.vector.tensor_reduce(
-                denom[:, 1], terms[:].rearrange("p q t u -> p q u t"), axis=AXIS.X, op=ALU.add, negate=True
-            )
+                    nc.scalar.activation(
+                        terms[:, 1, q, t, :],
+                        e[:, q, :],
+                        ACT.Exp,
+                        bias=e[:, q, t : t + 1],
+                        scale=-1.0,
+                        accum_out=denom[:, 1, q, t : t + 1],
+                    )
+            nc.scalar.activation(denom[:, 1], denom[:, 1], ACT.Copy, scale=-1.0)
             att = small.tile([P, SIGNS, NQ, K], F32, name="att")
             nc.vector.reciprocal(att[:], denom[:])
 

@@ -14,14 +14,17 @@ P = 128
 C, S, K, N = 256, 2048, 4, 8192
 BLOCKS = C // P
 SLOPE = 0.3
+SIGNS = 2
+BANK = 512
+
 PIECE = 2048
 PIECES = N // PIECE
 NODES = PIECE // K
+
 PER = PIECE // P
 NQ = PER // K
-SIGNS = 2
-PARK_ROWS = PIECE // NODES
-PARK_ROW0 = SIGNS * C - SIGNS * PARK_ROWS
+PARKED = 1 + SIGNS
+PARK_ROW0 = SIGNS * C - PIECES * PARKED
 
 FLOPS = 2 * C * N + 2 * C * S + SIGNS * 2 * C * N
 
@@ -30,15 +33,13 @@ def tile_signed_gat_kernel(tc, x, p_dst, p_src, offs, out):
     nc = tc.nc
     with ExitStack() as ctx:
         held = ctx.enter_context(tc.tile_pool(name="held", bufs=1))
-        prod_pool = ctx.enter_context(tc.tile_pool(name="prod", bufs=2))
-        small = ctx.enter_context(tc.tile_pool(name="small", bufs=2))
+        score_pool = ctx.enter_context(tc.tile_pool(name="score", bufs=2))
+        small = ctx.enter_context(tc.tile_pool(name="small", bufs=PIECES))
         weight_pool = ctx.enter_context(tc.tile_pool(name="weights", bufs=PIECES))
         picked_pool = ctx.enter_context(tc.tile_pool(name="picked", bufs=3))
         plane_pool = ctx.enter_context(tc.tile_pool(name="planes", bufs=3))
         result_pool = ctx.enter_context(tc.tile_pool(name="result", bufs=3))
-        psum_v = ctx.enter_context(tc.psum_pool(name="psum_v", bufs=2))
-        psum_e = ctx.enter_context(tc.psum_pool(name="psum_e", bufs=2))
-        psum_sum = ctx.enter_context(tc.psum_pool(name="psum_sum", bufs=4))
+        psum_bank = ctx.enter_context(tc.psum_pool(name="psum_bank", bufs=4))
 
         offsets = held.tile([P, N // 16], U16, name="offsets")
         nc.sync.dma_start(offsets[:], offs)
@@ -48,164 +49,118 @@ def tile_signed_gat_kernel(tc, x, p_dst, p_src, offs, out):
             nc.scalar.dma_start(src_w[:], p_src.rearrange("(b c) o -> c (b o)", b=BLOCKS))
             nc.scalar.dma_start(dst_w[:], p_dst.rearrange("(b c) o -> c (b o)", b=BLOCKS))
         table = [held.tile([P, S], F32, name=f"table{b}") for b in range(BLOCKS)]
-        nc.sync.dma_start(table[0][:], x[0:P, :])
-        nc.scalar.dma_start(table[1][:], x[P : 2 * P, :])
+        for n0 in range(0, S, BANK):
+            nc.sync.dma_start(table[0][:, n0 : n0 + BANK], x[0:P, n0 : n0 + BANK])
+            nc.scalar.dma_start(table[1][:, n0 : n0 + BANK], x[P : 2 * P, n0 : n0 + BANK])
 
         identity = held.tile([P, P], F32, name="identity")
         make_identity(nc, identity[:])
-        one_hot = held.tile([P, PER, PER], BF16, name="one_hot")
-        nc.gpsimd.memset(one_hot[:], 0.0)
-        for f in range(PER):
-            nc.gpsimd.memset(one_hot[:, f, f : f + 1], 1.0)
-        src_wide = [held.tile([P, PIECE], F32, name=f"src_wide{b}") for b in range(BLOCKS)]
-        for b in range(BLOCKS):
-            nc.vector.tensor_copy(src_wide[b][:], src_w[:, b : b + 1].to_broadcast([P, PIECE]))
-        dst_cols = held.tile([P, BLOCKS, NQ, PER], BF16, name="dst_cols")
-        nc.gpsimd.memset(dst_cols[:], 0.0)
-        for q in range(NQ):
-            nc.gpsimd.tensor_copy(
-                dst_cols[:, :, q, q * K : (q + 1) * K], dst_w[:].unsqueeze(2).to_broadcast([P, BLOCKS, K])
-            )
-        own = [held.tile([P, NQ, S // NQ], BF16, name=f"own{b}") for b in range(BLOCKS)]
-        for b in range(BLOCKS):
+        src_spread = held.tile([P, BLOCKS, P], BF16, name="src_spread")
+        nc.vector.tensor_copy(src_spread[:], src_w[:].unsqueeze(2).to_broadcast([P, BLOCKS, P]))
+        dst_spread = held.tile([P, BLOCKS, P], BF16, name="dst_spread")
+        nc.vector.tensor_copy(dst_spread[:], dst_w[:].unsqueeze(2).to_broadcast([P, BLOCKS, P]))
+        warm = held.tile([P, 1], F32, name="warm")
+        nc.scalar.activation(warm[:], identity[:, 0:1], ACT.Exp)
+
+        x_bf = [held.tile([P, S], BF16, name=f"x_bf{b}") for b in range(BLOCKS)]
+        as_neighbour = held.tile([P, S], F32, name="as_neighbour")
+        as_receiver = held.tile([P, S, K], F32, name="as_receiver")
+        for n0 in range(0, S, BANK):
+            nodes = slice(n0, n0 + BANK)
+            nc.vector.tensor_copy(x_bf[0][:, nodes], table[0][:, nodes])
+            nc.gpsimd.tensor_copy(x_bf[1][:, nodes], table[1][:, nodes])
+            src_sum = psum_bank.tile([P, BANK], F32, name="bank")
+            for b in range(BLOCKS):
+                nc.tensor.matmul(
+                    src_sum[:], lhsT=src_spread[:, b, :], rhs=x_bf[b][:, nodes], start=(b == 0), stop=(b == BLOCKS - 1)
+                )
+            nc.vector.tensor_copy(as_neighbour[:, nodes], src_sum[:])
+            dst_sum = psum_bank.tile([P, BANK], F32, name="bank")
+            for b in range(BLOCKS):
+                nc.tensor.matmul(
+                    dst_sum[:], lhsT=dst_spread[:, b, :], rhs=x_bf[b][:, nodes], start=(b == 0), stop=(b == BLOCKS - 1)
+                )
             nc.scalar.activation(
-                own[b][:].rearrange("c q n -> c n q"), table[b][:].rearrange("c (n q) -> c n q", q=NQ), ACT.Copy
+                as_receiver[:, nodes, :], dst_sum[:].unsqueeze(2).to_broadcast([P, BANK, K]), ACT.Copy
             )
 
         def piece_offsets(k):
             return offsets[:, k * (PIECE // 16) : (k + 1) * (PIECE // 16)]
 
         def attention_weights(k):
-            products = []
-            for b in range(BLOCKS):
-                prod = prod_pool.tile([P, PIECE], F32, name="prod")
-                nc.vector.tensor_tensor(
-                    prod[:],
-                    table[b][:].indirect(piece_offsets(k)),
-                    src_wide[b][:],
-                    ALU.mult,
-                )
-                prod_bf = prod_pool.tile([P, PER, P], BF16, name=f"prod_bf{b}")
-                for q in range(NQ):
-                    nc.scalar.activation(
-                        prod_bf[:, q * K : (q + 1) * K, :].rearrange("c t p -> c p t"),
-                        prod[:].rearrange("c (p f) -> c p f", f=PER)[:, :, q * K : (q + 1) * K],
-                        ACT.Copy,
-                    )
-                products.append(prod_bf)
-
-            v = psum_v.tile([P, NQ, K], F32, name="v")
-            v_flat = v[:].rearrange("p q t -> p (q t)")
-            for b in range(BLOCKS):
-                for q in range(NQ):
-                    nc.tensor.matmul(
-                        v_flat,
-                        lhsT=own[b][:, q, k * P : (k + 1) * P],
-                        rhs=dst_cols[:, b, q, :],
-                        start=(b == 0 and q == 0),
-                        stop=False,
-                    )
-            for b in range(BLOCKS):
-                for f in range(PER):
-                    nc.tensor.matmul(
-                        v_flat,
-                        lhsT=products[b][:, f, :],
-                        rhs=one_hot[:, f, :],
-                        start=False,
-                        stop=(b == BLOCKS - 1 and f == PER - 1),
-                    )
-
-            parts = small.tile([P, 2, PER], F32, name="parts")
-            nc.scalar.activation(parts[:, 0, :], v_flat, ACT.Relu, scale=1.0 - SLOPE)
-            nc.scalar.activation(parts[:, 1, :], v_flat, ACT.Copy, scale=SLOPE)
-            e_sum = psum_e.tile([P, NQ, K], F32, name="e_sum")
-            for h in range(2):
-                nc.tensor.matmul(
-                    e_sum[:].rearrange("p q t -> p (q t)"),
-                    lhsT=identity[:],
-                    rhs=parts[:, h, :],
-                    start=(h == 0),
-                    stop=(h == 1),
-                )
+            v_wide = score_pool.tile([P, PIECE], F32, name="v_wide")
+            nc.vector.tensor_tensor(
+                v_wide[:],
+                as_neighbour[:].indirect(piece_offsets(k)),
+                as_receiver[:, k * NODES : (k + 1) * NODES, :].rearrange("c i t -> c (i t)"),
+                ALU.add,
+            )
+            park = out[PARK_ROW0 + k * PARKED : PARK_ROW0 + (k + 1) * PARKED, :]
+            nc.sync.dma_start(park[0:1, :], v_wide[0:1, :])
+            v = small.tile([P, NQ, K], F32, name="v")
+            nc.sync.dma_start(
+                v[:].rearrange("p q t -> p (q t)"), park[0:1, :].rearrange("o (p f) -> (o p) f", f=PER)
+            )
             e = small.tile([P, NQ, K], F32, name="e")
-            nc.scalar.activation(e[:], e_sum[:], ACT.Copy)
-            minus_e = small.tile([P, NQ, K], F32, name="minus_e")
-            nc.scalar.activation(minus_e[:], e_sum[:], ACT.Copy, scale=-1.0)
-            denom = small.tile([P, SIGNS, NQ, K], F32, name="denom")
+            nc.vector.scalar_tensor_tensor(e[:], in0=v[:], scalar=SLOPE, in1=v[:], op0=ALU.mult, op1=ALU.max)
+            ahead = small.tile([P, NQ, K, K], F32, name="ahead")
+            nc.vector.tensor_tensor(
+                ahead[:],
+                e[:].unsqueeze(2).to_broadcast([P, NQ, K, K]),
+                e[:].unsqueeze(3).to_broadcast([P, NQ, K, K]),
+                ALU.subtract,
+            )
             terms = small.tile([P, SIGNS, NQ, K, K], F32, name="terms")
-            for q in range(NQ):
-                for t in range(K):
-                    nc.scalar.activation(
-                        terms[:, 0, q, t, :],
-                        e[:, q, :],
-                        ACT.Exp,
-                        bias=minus_e[:, q, t : t + 1],
-                        scale=1.0,
-                        accum_out=denom[:, 0, q, t : t + 1],
-                    )
-                    nc.scalar.activation(
-                        terms[:, 1, q, t, :],
-                        e[:, q, :],
-                        ACT.Exp,
-                        bias=e[:, q, t : t + 1],
-                        scale=-1.0,
-                        accum_out=denom[:, 1, q, t : t + 1],
-                    )
-            nc.scalar.activation(denom[:, 1], denom[:, 1], ACT.Copy, scale=-1.0)
+            nc.scalar.activation(terms[:, 0], ahead[:], ACT.Exp)
+            nc.scalar.activation(terms[:, 1], terms[:, 0].rearrange("p q t u -> p q u t"), ACT.Copy, scale=-1.0)
+            denom = small.tile([P, SIGNS, NQ, K], F32, name="denom")
+            nc.vector.tensor_reduce(
+                denom[:].rearrange("p s q t -> p (s q t)"),
+                terms[:].rearrange("p s q t u -> p (s q t) u"),
+                axis=AXIS.X,
+                op=ALU.add,
+            )
             att = small.tile([P, SIGNS, NQ, K], F32, name="att")
             nc.vector.reciprocal(att[:], denom[:])
-
-            park = out[PARK_ROW0 : PARK_ROW0 + SIGNS * PARK_ROWS, k * NODES : (k + 1) * NODES]
-            park_by_row = park.rearrange("(s h) (l f) -> h l s f", s=SIGNS, f=PER)
-            lanes = P // PARK_ROWS
-            for h in range(PARK_ROWS):
-                nc.sync.dma_start(
-                    park_by_row[h],
-                    att[h * lanes : (h + 1) * lanes].rearrange("l s q t -> l s (q t)"),
-                )
-            weights = weight_pool.tile([P, SIGNS, PIECE], F32, name="weights")
+            nc.sync.dma_start(
+                park[1:PARKED, :].rearrange("s (p f) -> p s f", f=PER), att[:].rearrange("p s q t -> p s (q t)")
+            )
+            wide = weight_pool.tile([P, SIGNS, PIECE], F32, name="wide")
             for s in range(SIGNS):
-                nc.sync.dma_start(
-                    weights[:, s, :].rearrange("c (h w) -> c h w", w=NODES),
-                    park[s * PARK_ROWS : (s + 1) * PARK_ROWS, :]
-                    .unsqueeze(0)
-                    .to_broadcast([P, PARK_ROWS, NODES]),
-                )
-            return weights
+                nc.sync.dma_start(wide[:, s, :], park[1 + s : 2 + s, :].to_broadcast([P, PIECE]))
+            return wide
 
-        def weighted_sums(k, weights):
+        def weighted_sums(k):
             for s in range(SIGNS):
                 for b in range(BLOCKS):
                     picked = picked_pool.tile([P, PIECE], F32, name="picked")
                     nc.vector.tensor_tensor(
-                        picked[:], table[b][:].indirect(piece_offsets(k)), weights[:, s, :], ALU.mult
+                        picked[:],
+                        table[b][:].indirect(piece_offsets(k)),
+                        weights[k][:, s, :],
+                        ALU.mult,
                     )
                     result = result_pool.tile([P, NODES], F32, name="result")
-                    row0 = (s * BLOCKS + b) * P
                     if k == PIECES - 1 and s == SIGNS - 1 and b == BLOCKS - 1:
                         nc.vector.tensor_reduce(
                             result[:], picked[:].rearrange("c (i t) -> c i t", t=K), axis=AXIS.X, op=ALU.add
                         )
-                        nc.sync.dma_start(out[row0 : row0 + P, k * NODES : (k + 1) * NODES], result[:])
-                        continue
-                    planes = plane_pool.tile([P, K, NODES], F32, name="planes")
-                    nc.scalar.activation(
-                        planes[:].rearrange("c t i -> c i t"),
-                        picked[:].rearrange("c (i t) -> c i t", t=K),
-                        ACT.Copy,
-                    )
-                    total = psum_sum.tile([P, NODES], F32, name="total")
-                    for t in range(K):
-                        nc.tensor.matmul(
-                            total[:],
-                            lhsT=identity[:],
-                            rhs=planes[:, t, :],
-                            start=(t == 0),
-                            stop=(t == K - 1),
+                    else:
+                        planes = plane_pool.tile([P, K, NODES], F32, name="planes")
+                        nc.scalar.activation(
+                            planes[:].rearrange("c t i -> c i t"),
+                            picked[:].rearrange("c (i t) -> c i t", t=K),
+                            ACT.Copy,
                         )
-                    nc.scalar.activation(result[:], total[:], ACT.Copy)
-                    nc.scalar.dma_start(out[row0 : row0 + P, k * NODES : (k + 1) * NODES], result[:])
+                        total = psum_bank.tile([P, NODES], F32, name="bank")
+                        for t in range(K):
+                            nc.tensor.matmul(
+                                total[:], lhsT=identity[:], rhs=planes[:, t, :], start=(t == 0), stop=(t == K - 1)
+                            )
+                        nc.scalar.activation(result[:], total[:], ACT.Copy)
+                    row0 = (s * BLOCKS + b) * P
+                    nc.sync.dma_start(out[row0 : row0 + P, k * NODES : (k + 1) * NODES], result[:])
 
         weights = [attention_weights(k) for k in range(PIECES)]
         for k in range(PIECES):
-            weighted_sums(k, weights[k])
+            weighted_sums(k)

@@ -19,8 +19,10 @@ BANK = 512
 
 PIECE = 2048
 PIECES = N // PIECE
-NODES = PIECE // K
+TILE = 1024
+NODES = TILE // K
 
+STEP = 512
 PER = PIECE // P
 NQ = PER // K
 PARKED = 1 + SIGNS
@@ -36,10 +38,10 @@ def tile_signed_gat_kernel(tc, x, p_dst, p_src, offs, out):
         score_pool = ctx.enter_context(tc.tile_pool(name="score", bufs=2))
         small = ctx.enter_context(tc.tile_pool(name="small", bufs=PIECES))
         weight_pool = ctx.enter_context(tc.tile_pool(name="weights", bufs=PIECES))
-        picked_pool = ctx.enter_context(tc.tile_pool(name="picked", bufs=3))
-        plane_pool = ctx.enter_context(tc.tile_pool(name="planes", bufs=3))
-        result_pool = ctx.enter_context(tc.tile_pool(name="result", bufs=3))
-        psum_bank = ctx.enter_context(tc.psum_pool(name="psum_bank", bufs=4))
+        picked_pool = ctx.enter_context(tc.tile_pool(name="picked", bufs=6))
+        plane_pool = ctx.enter_context(tc.tile_pool(name="planes", bufs=6))
+        result_pool = ctx.enter_context(tc.tile_pool(name="result", bufs=6))
+        psum_bank = ctx.enter_context(tc.psum_pool(name="psum_bank", bufs=8))
 
         offsets = held.tile([P, N // 16], U16, name="offsets")
         nc.sync.dma_start(offsets[:], offs)
@@ -84,25 +86,25 @@ def tile_signed_gat_kernel(tc, x, p_dst, p_src, offs, out):
                 as_receiver[:, nodes, :], dst_sum[:].unsqueeze(2).to_broadcast([P, BANK, K]), ACT.Copy
             )
 
-        def piece_offsets(k):
-            return offsets[:, k * (PIECE // 16) : (k + 1) * (PIECE // 16)]
-
         def attention_weights(k):
-            v_wide = score_pool.tile([P, PIECE], F32, name="v_wide")
-            nc.vector.tensor_tensor(
-                v_wide[:],
-                as_neighbour[:].indirect(piece_offsets(k)),
-                as_receiver[:, k * NODES : (k + 1) * NODES, :].rearrange("c i t -> c (i t)"),
-                ALU.add,
-            )
+            v_both = score_pool.tile([P, PIECE + PER], F32, name="v_both")
+            v_wide = v_both[:, 0:PIECE]
+            v = v_both[:, PIECE : PIECE + PER].rearrange("p (q t) -> p q t", t=K)
+            for j0 in range(0, PIECE, STEP):
+                first = k * PIECE + j0
+                nc.vector.tensor_tensor(
+                    v_wide[:, j0 : j0 + STEP],
+                    as_neighbour[:].indirect(offsets[:, first // 16 : (first + STEP) // 16]),
+                    as_receiver[:, first // K : (first + STEP) // K, :].rearrange("c i t -> c (i t)"),
+                    ALU.add,
+                )
             park = out[PARK_ROW0 + k * PARKED : PARK_ROW0 + (k + 1) * PARKED, :]
-            nc.sync.dma_start(park[0:1, :], v_wide[0:1, :])
-            v = small.tile([P, NQ, K], F32, name="v")
+            nc.sync.dma_start(park[0:1, :], v_both[0:1, 0:PIECE])
             nc.sync.dma_start(
-                v[:].rearrange("p q t -> p (q t)"), park[0:1, :].rearrange("o (p f) -> (o p) f", f=PER)
+                v_both[:, PIECE : PIECE + PER], park[0:1, :].rearrange("o (p f) -> (o p) f", f=PER)
             )
             e = small.tile([P, NQ, K], F32, name="e")
-            nc.vector.scalar_tensor_tensor(e[:], in0=v[:], scalar=SLOPE, in1=v[:], op0=ALU.mult, op1=ALU.max)
+            nc.vector.scalar_tensor_tensor(e[:], in0=v, scalar=SLOPE, in1=v, op0=ALU.mult, op1=ALU.max)
             ahead = small.tile([P, NQ, K, K], F32, name="ahead")
             nc.vector.tensor_tensor(
                 ahead[:],
@@ -130,37 +132,36 @@ def tile_signed_gat_kernel(tc, x, p_dst, p_src, offs, out):
                 nc.sync.dma_start(wide[:, s, :], park[1 + s : 2 + s, :].to_broadcast([P, PIECE]))
             return wide
 
-        def weighted_sums(k):
-            for s in range(SIGNS):
-                for b in range(BLOCKS):
-                    picked = picked_pool.tile([P, PIECE], F32, name="picked")
-                    nc.vector.tensor_tensor(
-                        picked[:],
-                        table[b][:].indirect(piece_offsets(k)),
-                        weights[k][:, s, :],
-                        ALU.mult,
+        def weighted_sum(first, s, b, is_last):
+            picked = picked_pool.tile([P, TILE], F32, name="picked")
+            nc.vector.tensor_tensor(
+                picked[:],
+                table[b][:].indirect(offsets[:, first // 16 : (first + TILE) // 16]),
+                weights[first // PIECE][:, s, first % PIECE : first % PIECE + TILE],
+                ALU.mult,
+            )
+            result = result_pool.tile([P, NODES], F32, name="result")
+            stored = out[(s * BLOCKS + b) * P : (s * BLOCKS + b + 1) * P, first // K : first // K + NODES]
+            if is_last:
+                nc.vector.tensor_reduce(
+                    result[:], picked[:].rearrange("c (i t) -> c i t", t=K), axis=AXIS.X, op=ALU.add
+                )
+                nc.sync.dma_start(stored, result[:])
+            else:
+                planes = plane_pool.tile([P, K, NODES], F32, name="planes")
+                nc.scalar.activation(
+                    planes[:].rearrange("c t i -> c i t"), picked[:].rearrange("c (i t) -> c i t", t=K), ACT.Copy
+                )
+                total = psum_bank.tile([P, NODES], F32, name="bank")
+                for t in range(K):
+                    nc.tensor.matmul(
+                        total[:], lhsT=identity[:], rhs=planes[:, t, :], start=(t == 0), stop=(t == K - 1)
                     )
-                    result = result_pool.tile([P, NODES], F32, name="result")
-                    if k == PIECES - 1 and s == SIGNS - 1 and b == BLOCKS - 1:
-                        nc.vector.tensor_reduce(
-                            result[:], picked[:].rearrange("c (i t) -> c i t", t=K), axis=AXIS.X, op=ALU.add
-                        )
-                    else:
-                        planes = plane_pool.tile([P, K, NODES], F32, name="planes")
-                        nc.scalar.activation(
-                            planes[:].rearrange("c t i -> c i t"),
-                            picked[:].rearrange("c (i t) -> c i t", t=K),
-                            ACT.Copy,
-                        )
-                        total = psum_bank.tile([P, NODES], F32, name="bank")
-                        for t in range(K):
-                            nc.tensor.matmul(
-                                total[:], lhsT=identity[:], rhs=planes[:, t, :], start=(t == 0), stop=(t == K - 1)
-                            )
-                        nc.scalar.activation(result[:], total[:], ACT.Copy)
-                    row0 = (s * BLOCKS + b) * P
-                    nc.sync.dma_start(out[row0 : row0 + P, k * NODES : (k + 1) * NODES], result[:])
+                nc.scalar.activation(result[:], total[:], ACT.Copy)
+                nc.scalar.dma_start(stored, result[:])
 
         weights = [attention_weights(k) for k in range(PIECES)]
-        for k in range(PIECES):
-            weighted_sums(k)
+        for first in range(0, N, TILE):
+            for s in range(SIGNS):
+                for b in range(BLOCKS):
+                    weighted_sum(first, s, b, is_last=(first == N - TILE and s == SIGNS - 1 and b == BLOCKS - 1))

@@ -146,7 +146,6 @@ def tile_signed_gat_kernel(tc, x, p_dst, p_src, offs, out):
                 nc.vector.tensor_reduce(
                     result[:], picked[:].rearrange("c (i t) -> c i t", t=K), axis=AXIS.X, op=ALU.add
                 )
-                nc.sync.dma_start(stored, result[:])
             else:
                 planes = plane_pool.tile([P, K, NODES], F32, name="planes")
                 nc.scalar.activation(
@@ -158,7 +157,7 @@ def tile_signed_gat_kernel(tc, x, p_dst, p_src, offs, out):
                         total[:], lhsT=identity[:], rhs=planes[:, t, :], start=(t == 0), stop=(t == K - 1)
                     )
                 nc.scalar.activation(result[:], total[:], ACT.Copy)
-                nc.scalar.dma_start(stored, result[:])
+            nc.sync.dma_start(stored, result[:])
 
         weights = [attention_weights(k) for k in range(PIECES)]
         for first in range(0, N, TILE):

@@ -61,8 +61,6 @@ def tile_signed_gat_kernel(tc, x, p_dst, p_src, offs, out):
         nc.vector.tensor_copy(src_spread[:], src_w[:].unsqueeze(2).to_broadcast([P, BLOCKS, P]))
         dst_spread = held.tile([P, BLOCKS, P], BF16, name="dst_spread")
         nc.vector.tensor_copy(dst_spread[:], dst_w[:].unsqueeze(2).to_broadcast([P, BLOCKS, P]))
-        warm = held.tile([P, 1], F32, name="warm")
-        nc.scalar.activation(warm[:], identity[:, 0:1], ACT.Exp)
 
         x_bf = [held.tile([P, S], BF16, name=f"x_bf{b}") for b in range(BLOCKS)]
         as_neighbour = held.tile([P, S], F32, name="as_neighbour")

@@ -17,16 +17,17 @@ SLOPE = 0.3
 SIGNS = 2
 BANK = 512
 
-PIECE = 2048
-PIECES = N // PIECE
-TILE = 1024
-NODES = TILE // K
-
-STEP = 512
-PER = PIECE // P
+UNIT = 1024
+NODES = UNIT // K
+PER = UNIT // P
 NQ = PER // K
+STEP = UNIT // 2
+UNITS = N // UNIT
+PIECES = (range(0, 1), range(1, UNITS // 2), range(UNITS // 2, UNITS))
+GROUP = 2
+
+PARK_COL = S - UNIT
 PARKED = 1 + SIGNS
-PARK_ROW0 = SIGNS * C - PIECES * PARKED
 
 FLOPS = 2 * C * N + 2 * C * S + SIGNS * 2 * C * N
 
@@ -35,13 +36,13 @@ def tile_signed_gat_kernel(tc, x, p_dst, p_src, offs, out):
     nc = tc.nc
     with ExitStack() as ctx:
         held = ctx.enter_context(tc.tile_pool(name="held", bufs=1))
-        score_pool = ctx.enter_context(tc.tile_pool(name="score", bufs=2))
-        small = ctx.enter_context(tc.tile_pool(name="small", bufs=PIECES))
-        weight_pool = ctx.enter_context(tc.tile_pool(name="weights", bufs=PIECES))
+        score_pool = ctx.enter_context(tc.tile_pool(name="score", bufs=1))
+        small = ctx.enter_context(tc.tile_pool(name="small", bufs=len(PIECES)))
         picked_pool = ctx.enter_context(tc.tile_pool(name="picked", bufs=6))
         plane_pool = ctx.enter_context(tc.tile_pool(name="planes", bufs=6))
         result_pool = ctx.enter_context(tc.tile_pool(name="result", bufs=6))
-        psum_bank = ctx.enter_context(tc.psum_pool(name="psum_bank", bufs=8))
+        psum_bank = ctx.enter_context(tc.psum_pool(name="psum_bank", bufs=7))
+        psum_receiver = ctx.enter_context(tc.psum_pool(name="psum_receiver", bufs=1))
 
         offsets = held.tile([P, N // 16], U16, name="offsets")
         nc.sync.dma_start(offsets[:], offs)
@@ -65,84 +66,119 @@ def tile_signed_gat_kernel(tc, x, p_dst, p_src, offs, out):
         x_bf = [held.tile([P, S], BF16, name=f"x_bf{b}") for b in range(BLOCKS)]
         as_neighbour = held.tile([P, S], F32, name="as_neighbour")
         as_receiver = held.tile([P, S, K], F32, name="as_receiver")
-        for n0 in range(0, S, BANK):
+
+        def round_part(n0):
             nodes = slice(n0, n0 + BANK)
             nc.vector.tensor_copy(x_bf[0][:, nodes], table[0][:, nodes])
-            nc.gpsimd.tensor_copy(x_bf[1][:, nodes], table[1][:, nodes])
-            src_sum = psum_bank.tile([P, BANK], F32, name="bank")
-            for b in range(BLOCKS):
-                nc.tensor.matmul(
-                    src_sum[:], lhsT=src_spread[:, b, :], rhs=x_bf[b][:, nodes], start=(b == 0), stop=(b == BLOCKS - 1)
-                )
-            nc.vector.tensor_copy(as_neighbour[:, nodes], src_sum[:])
-            dst_sum = psum_bank.tile([P, BANK], F32, name="bank")
-            for b in range(BLOCKS):
-                nc.tensor.matmul(
-                    dst_sum[:], lhsT=dst_spread[:, b, :], rhs=x_bf[b][:, nodes], start=(b == 0), stop=(b == BLOCKS - 1)
-                )
-            nc.scalar.activation(
-                as_receiver[:, nodes, :], dst_sum[:].unsqueeze(2).to_broadcast([P, BANK, K]), ACT.Copy
-            )
+            second = nc.vector if n0 == S - BANK else nc.gpsimd
+            second.tensor_copy(x_bf[1][:, nodes], table[1][:, nodes])
 
-        def attention_weights(k):
-            v_both = score_pool.tile([P, PIECE + PER], F32, name="v_both")
-            v_wide = v_both[:, 0:PIECE]
-            v = v_both[:, PIECE : PIECE + PER].rearrange("p (q t) -> p q t", t=K)
-            for j0 in range(0, PIECE, STEP):
-                first = k * PIECE + j0
+        def sum_over_c(total, spread, n0):
+            for b in range(BLOCKS):
+                nc.tensor.matmul(
+                    total[:],
+                    lhsT=spread[:, b, :],
+                    rhs=x_bf[b][:, n0 : n0 + BANK],
+                    start=(b == 0),
+                    stop=(b == BLOCKS - 1),
+                )
+
+        def neighbours(n0):
+            src_sum = psum_bank.tile([P, BANK], F32, name="bank")
+            sum_over_c(src_sum, src_spread, n0)
+            nc.vector.tensor_copy(as_neighbour[:, n0 : n0 + BANK], src_sum[:])
+
+        def receivers(n0):
+            dst_sum = psum_receiver.tile([P, BANK], F32, name="receiver")
+            sum_over_c(dst_sum, dst_spread, n0)
+            for i0 in range(0, BANK, STEP // K):
+                nc.scalar.activation(
+                    as_receiver[:, n0 + i0 : n0 + i0 + STEP // K, :],
+                    dst_sum[:, i0 : i0 + STEP // K].unsqueeze(2).to_broadcast([P, STEP // K, K]),
+                    ACT.Copy,
+                )
+
+        for n0 in range(0, S, BANK):
+            round_part(n0)
+            neighbours(n0)
+            receivers(n0)
+
+        parked_scores = out[0:UNITS, PARK_COL : PARK_COL + UNIT]
+        parked_weights = out[UNITS : PARKED * UNITS, PARK_COL : PARK_COL + UNIT]
+
+        def queue_of(unit):
+            return nc.gpsimd if unit in PIECES[2] else nc.sync
+
+        def look_up_scores(group):
+            scores = score_pool.tile([P, GROUP * UNIT + UNITS * PER], F32, name=f"scores{group % 2}")
+            for j0 in range(0, GROUP * UNIT, STEP):
+                first = group * GROUP * UNIT + j0
                 nc.vector.tensor_tensor(
-                    v_wide[:, j0 : j0 + STEP],
+                    scores[:, j0 : j0 + STEP],
                     as_neighbour[:].indirect(offsets[:, first // 16 : (first + STEP) // 16]),
                     as_receiver[:, first // K : (first + STEP) // K, :].rearrange("c i t -> c (i t)"),
                     ALU.add,
                 )
-            park = out[PARK_ROW0 + k * PARKED : PARK_ROW0 + (k + 1) * PARKED, :]
-            nc.sync.dma_start(park[0:1, :], v_both[0:1, 0:PIECE])
-            nc.sync.dma_start(
-                v_both[:, PIECE : PIECE + PER], park[0:1, :].rearrange("o (p f) -> (o p) f", f=PER)
+                if (j0 + STEP) % UNIT == 0:
+                    u0 = j0 + STEP - UNIT
+                    row = group * GROUP + u0 // UNIT
+                    store_queue = nc.sync if row == 0 else nc.gpsimd
+                    store_queue.dma_start(parked_scores[row : row + 1, :], scores[0:1, u0 : u0 + UNIT])
+            return scores[:, GROUP * UNIT :]
+
+        def attention_weights(piece, room):
+            units = len(piece)
+            nq = units * NQ
+            queue = queue_of(piece.start)
+            v_flat = room[:, 0 : units * PER]
+            queue.dma_start(
+                v_flat.rearrange("p (u f) -> p u f", f=PER),
+                parked_scores[piece.start : piece.stop, :].rearrange("u (p f) -> p u f", f=PER),
             )
-            e = small.tile([P, NQ, K], F32, name="e")
+            v = v_flat.rearrange("p (q t) -> p q t", t=K)
+            e = small.tile([P, nq, K], F32, name="e")
             nc.vector.scalar_tensor_tensor(e[:], in0=v, scalar=SLOPE, in1=v, op0=ALU.mult, op1=ALU.max)
-            ahead = small.tile([P, NQ, K, K], F32, name="ahead")
+            ahead = small.tile([P, nq, K, K], F32, name="ahead")
             nc.vector.tensor_tensor(
                 ahead[:],
-                e[:].unsqueeze(2).to_broadcast([P, NQ, K, K]),
-                e[:].unsqueeze(3).to_broadcast([P, NQ, K, K]),
+                e[:].unsqueeze(2).to_broadcast([P, nq, K, K]),
+                e[:].unsqueeze(3).to_broadcast([P, nq, K, K]),
                 ALU.subtract,
             )
-            terms = small.tile([P, SIGNS, NQ, K, K], F32, name="terms")
-            nc.scalar.activation(terms[:, 0], ahead[:], ACT.Exp)
-            nc.scalar.activation(terms[:, 1], terms[:, 0].rearrange("p q t u -> p q u t"), ACT.Copy, scale=-1.0)
-            denom = small.tile([P, SIGNS, NQ, K], F32, name="denom")
+            terms = small.tile([P, nq, K, K], F32, name="terms")
+            nc.scalar.activation(terms[:], ahead[:], ACT.Exp)
+            denom = small.tile([P, SIGNS, nq, K], F32, name="denom")
+            nc.vector.tensor_reduce(denom[:, 0], terms[:], axis=AXIS.X, op=ALU.add)
             nc.vector.tensor_reduce(
-                denom[:].rearrange("p s q t -> p (s q t)"),
-                terms[:].rearrange("p s q t u -> p (s q t) u"),
-                axis=AXIS.X,
-                op=ALU.add,
+                denom[:, 1], terms[:].rearrange("p q t u -> p q u t"), axis=AXIS.X, op=ALU.add, negate=True
             )
-            att = small.tile([P, SIGNS, NQ, K], F32, name="att")
+            att = small.tile([P, SIGNS, nq, K], F32, name="att")
             nc.vector.reciprocal(att[:], denom[:])
-            nc.sync.dma_start(
-                park[1:PARKED, :].rearrange("s (p f) -> p s f", f=PER), att[:].rearrange("p s q t -> p s (q t)")
+            rows = parked_weights[SIGNS * piece.start : SIGNS * piece.stop, :]
+            queue.dma_start(
+                rows.rearrange("r (p f) -> p r f", f=PER),
+                att[:].rearrange("p s (u q) t -> p (s u) (q t)", q=NQ),
             )
-            wide = weight_pool.tile([P, SIGNS, PIECE], F32, name="wide")
-            for s in range(SIGNS):
-                nc.sync.dma_start(wide[:, s, :], park[1 + s : 2 + s, :].to_broadcast([P, PIECE]))
-            return wide
+            wides = []
+            for u in range(units):
+                wide = held.tile([P, SIGNS, UNIT], F32, name=f"wide{piece.start + u}")
+                for s in range(SIGNS):
+                    row = s * units + u
+                    queue.dma_start(wide[:, s, :], rows[row : row + 1, :].to_broadcast([P, UNIT]))
+                wides.append(wide)
+            return wides
 
-        def weighted_sum(first, s, b, is_last):
-            picked = picked_pool.tile([P, TILE], F32, name="picked")
+        def weighted_sum(result, a, unit, b, is_last):
+            picked = picked_pool.tile([P, UNIT], F32, name="picked")
             nc.vector.tensor_tensor(
                 picked[:],
-                table[b][:].indirect(offsets[:, first // 16 : (first + TILE) // 16]),
-                weights[first // PIECE][:, s, first % PIECE : first % PIECE + TILE],
+                table[b][:].indirect(offsets[:, unit * UNIT // 16 : (unit + 1) * UNIT // 16]),
+                a,
                 ALU.mult,
             )
-            result = result_pool.tile([P, NODES], F32, name="result")
-            stored = out[(s * BLOCKS + b) * P : (s * BLOCKS + b + 1) * P, first // K : first // K + NODES]
             if is_last:
                 nc.vector.tensor_reduce(
-                    result[:], picked[:].rearrange("c (i t) -> c i t", t=K), axis=AXIS.X, op=ALU.add
+                    result, picked[:].rearrange("c (i t) -> c i t", t=K), axis=AXIS.X, op=ALU.add
                 )
             else:
                 planes = plane_pool.tile([P, K, NODES], F32, name="planes")
@@ -154,11 +190,18 @@ def tile_signed_gat_kernel(tc, x, p_dst, p_src, offs, out):
                     nc.tensor.matmul(
                         total[:], lhsT=identity[:], rhs=planes[:, t, :], start=(t == 0), stop=(t == K - 1)
                     )
-                nc.scalar.activation(result[:], total[:], ACT.Copy)
-            nc.sync.dma_start(stored, result[:])
+                nc.scalar.activation(result, total[:], ACT.Copy)
 
-        weights = [attention_weights(k) for k in range(PIECES)]
-        for first in range(0, N, TILE):
+        rooms = [look_up_scores(group) for group in range(2)]
+        weights = attention_weights(PIECES[0], rooms[0]) + attention_weights(PIECES[1], rooms[1])
+        rooms = [look_up_scores(group) for group in range(2, UNITS // GROUP)]
+        weights += attention_weights(PIECES[2], rooms[-1])
+
+        for unit, wide in enumerate(weights):
             for s in range(SIGNS):
+                results = result_pool.tile([P, BLOCKS, NODES], F32, name="results")
                 for b in range(BLOCKS):
-                    weighted_sum(first, s, b, is_last=(first == N - TILE and s == SIGNS - 1 and b == BLOCKS - 1))
+                    is_last = unit == UNITS - 1 and s == SIGNS - 1 and b == BLOCKS - 1
+                    weighted_sum(results[:, b, :], wide[:, s, :], unit, b, is_last)
+                stored = out[s * C : (s + 1) * C, unit * NODES : (unit + 1) * NODES]
+                nc.sync.dma_start(stored.rearrange("(b c) i -> c b i", b=BLOCKS), results[:])

@@ -24,10 +24,7 @@ NQ = PER // K
 STEP = UNIT // 2
 UNITS = N // UNIT
 PIECES = (range(0, 1), range(1, UNITS // 2), range(UNITS // 2, UNITS))
-GROUP = 2
 
-PARK_COL = S - UNIT
-PARKED = 1 + SIGNS
 
 FLOPS = 2 * C * N + 2 * C * S + SIGNS * 2 * C * N
 
@@ -38,7 +35,7 @@ def tile_signed_gat_kernel(tc, x, p_dst, p_src, offs, out):
         held = ctx.enter_context(tc.tile_pool(name="held", bufs=1))
         score_pool = ctx.enter_context(tc.tile_pool(name="score", bufs=1))
         small = ctx.enter_context(tc.tile_pool(name="small", bufs=len(PIECES)))
-        picked_pool = ctx.enter_context(tc.tile_pool(name="picked", bufs=6))
+        picked_pool = ctx.enter_context(tc.tile_pool(name="picked", bufs=2))
         plane_pool = ctx.enter_context(tc.tile_pool(name="planes", bufs=6))
         result_pool = ctx.enter_context(tc.tile_pool(name="result", bufs=6))
         psum_bank = ctx.enter_context(tc.psum_pool(name="psum_bank", bufs=7))
@@ -103,68 +100,64 @@ def tile_signed_gat_kernel(tc, x, p_dst, p_src, offs, out):
             neighbours(n0)
             receivers(n0)
 
-        parked_scores = out[0:UNITS, PARK_COL : PARK_COL + UNIT]
-        parked_weights = out[UNITS : PARKED * UNITS, PARK_COL : PARK_COL + UNIT]
+        parked_scores = out[0:UNITS, 0:UNIT]
+        parked_weights = [out[s * C + UNITS : s * C + 2 * UNITS, 0:UNIT] for s in range(SIGNS)]
 
-        def queue_of(unit):
-            return nc.gpsimd if unit in PIECES[2] else nc.sync
-
-        def look_up_scores(group):
-            scores = score_pool.tile([P, GROUP * UNIT + UNITS * PER], F32, name=f"scores{group % 2}")
-            for j0 in range(0, GROUP * UNIT, STEP):
-                first = group * GROUP * UNIT + j0
+        def look_up_scores(units, tag, parks, queue):
+            scores = score_pool.tile([P, len(units) * UNIT], F32, name=tag)
+            for first in range(units.start * UNIT, units.stop * UNIT, STEP):
+                j0 = first - units.start * UNIT
                 nc.vector.tensor_tensor(
                     scores[:, j0 : j0 + STEP],
                     as_neighbour[:].indirect(offsets[:, first // 16 : (first + STEP) // 16]),
                     as_receiver[:, first // K : (first + STEP) // K, :].rearrange("c i t -> c (i t)"),
                     ALU.add,
                 )
-                if (j0 + STEP) % UNIT == 0:
-                    u0 = j0 + STEP - UNIT
-                    row = group * GROUP + u0 // UNIT
-                    store_queue = nc.sync if row == 0 else nc.gpsimd
-                    store_queue.dma_start(parked_scores[row : row + 1, :], scores[0:1, u0 : u0 + UNIT])
-            return scores[:, GROUP * UNIT :]
+            for run in parks:
+                j0 = (run.start - units.start) * UNIT
+                queue.dma_start(
+                    parked_scores[run.start : run.stop, :].unsqueeze(0),
+                    scores[0:1, j0 : j0 + len(run) * UNIT].rearrange("o (u e) -> o u e", e=UNIT),
+                )
 
-        def attention_weights(piece, room):
+        def attention_weights(piece, e_tag, denom_tag):
             units = len(piece)
             nq = units * NQ
-            queue = queue_of(piece.start)
-            v_flat = room[:, 0 : units * PER]
-            queue.dma_start(
-                v_flat.rearrange("p (u f) -> p u f", f=PER),
+            v_and_e = score_pool.tile([P, 2, nq, K], F32, name=e_tag)
+            v, e = v_and_e[:, 0], v_and_e[:, 1]
+            nc.sync.dma_start(
+                v.rearrange("p (u q) t -> p u (q t)", q=NQ),
                 parked_scores[piece.start : piece.stop, :].rearrange("u (p f) -> p u f", f=PER),
             )
-            v = v_flat.rearrange("p (q t) -> p q t", t=K)
-            e = small.tile([P, nq, K], F32, name="e")
-            nc.vector.scalar_tensor_tensor(e[:], in0=v, scalar=SLOPE, in1=v, op0=ALU.mult, op1=ALU.max)
+            nc.vector.scalar_tensor_tensor(e, in0=v, scalar=SLOPE, in1=v, op0=ALU.mult, op1=ALU.max)
             ahead = small.tile([P, nq, K, K], F32, name="ahead")
             nc.vector.tensor_tensor(
                 ahead[:],
-                e[:].unsqueeze(2).to_broadcast([P, nq, K, K]),
-                e[:].unsqueeze(3).to_broadcast([P, nq, K, K]),
+                e.unsqueeze(2).to_broadcast([P, nq, K, K]),
+                e.unsqueeze(3).to_broadcast([P, nq, K, K]),
                 ALU.subtract,
             )
             terms = small.tile([P, nq, K, K], F32, name="terms")
             nc.scalar.activation(terms[:], ahead[:], ACT.Exp)
-            denom = small.tile([P, SIGNS, nq, K], F32, name="denom")
+            denom = score_pool.tile([P, SIGNS, nq, K], F32, name=denom_tag)
             nc.vector.tensor_reduce(denom[:, 0], terms[:], axis=AXIS.X, op=ALU.add)
             nc.vector.tensor_reduce(
                 denom[:, 1], terms[:].rearrange("p q t u -> p q u t"), axis=AXIS.X, op=ALU.add, negate=True
             )
             att = small.tile([P, SIGNS, nq, K], F32, name="att")
             nc.vector.reciprocal(att[:], denom[:])
-            rows = parked_weights[SIGNS * piece.start : SIGNS * piece.stop, :]
-            queue.dma_start(
-                rows.rearrange("r (p f) -> p r f", f=PER),
-                att[:].rearrange("p s (u q) t -> p (s u) (q t)", q=NQ),
-            )
+            for s in range(SIGNS):
+                nc.sync.dma_start(
+                    parked_weights[s][piece.start : piece.stop, :].rearrange("u (p f) -> p u f", f=PER),
+                    att[:, s].rearrange("p (u q) t -> p u (q t)", q=NQ),
+                )
             wides = []
-            for u in range(units):
-                wide = held.tile([P, SIGNS, UNIT], F32, name=f"wide{piece.start + u}")
+            for unit in piece:
+                wide = score_pool.tile([P, SIGNS, UNIT], F32, name=f"wide{unit}")
                 for s in range(SIGNS):
-                    row = s * units + u
-                    queue.dma_start(wide[:, s, :], rows[row : row + 1, :].to_broadcast([P, UNIT]))
+                    nc.sync.dma_start(
+                        wide[:, s, :], parked_weights[s][unit : unit + 1, :].to_broadcast([P, UNIT])
+                    )
                 wides.append(wide)
             return wides
 
@@ -192,10 +185,13 @@ def tile_signed_gat_kernel(tc, x, p_dst, p_src, offs, out):
                     )
                 nc.scalar.activation(result, total[:], ACT.Copy)
 
-        rooms = [look_up_scores(group) for group in range(2)]
-        weights = attention_weights(PIECES[0], rooms[0]) + attention_weights(PIECES[1], rooms[1])
-        rooms = [look_up_scores(group) for group in range(2, UNITS // GROUP)]
-        weights += attention_weights(PIECES[2], rooms[-1])
+        look_up_scores(range(0, 4), "scores_0_to_3", parks=(PIECES[0], PIECES[1]), queue=nc.sync)
+        weights = attention_weights(PIECES[0], "scores_4", "scores_5_to_6")
+        look_up_scores(range(4, 5), "scores_4", parks=(range(4, 5),), queue=nc.sync)
+        look_up_scores(range(5, 7), "scores_5_to_6", parks=(range(5, 7),), queue=nc.gpsimd)
+        weights += attention_weights(PIECES[1], "scores_7", "denom_1")
+        look_up_scores(range(7, 8), "scores_7", parks=(range(7, 8),), queue=nc.gpsimd)
+        weights += attention_weights(PIECES[2], "e_2", "denom_2")
 
         for unit, wide in enumerate(weights):
             for s in range(SIGNS):

@@ -25,6 +25,8 @@ STEP = UNIT // 2
 UNITS = N // UNIT
 PIECES = (range(0, 1), range(1, UNITS // 2), range(UNITS // 2, UNITS))
 
+WEIGHT_ROW0, ROWS_OF_UNIT = UNITS, 3
+SCORE_ROW = [unit if unit < 4 else unit - 5 + WEIGHT_ROW0 for unit in range(UNITS)]
 
 FLOPS = 2 * C * N + 2 * C * S + SIGNS * 2 * C * N
 
@@ -36,22 +38,22 @@ def tile_signed_gat_kernel(tc, x, p_dst, p_src, offs, out):
         score_pool = ctx.enter_context(tc.tile_pool(name="score", bufs=1))
         small = ctx.enter_context(tc.tile_pool(name="small", bufs=len(PIECES)))
         picked_pool = ctx.enter_context(tc.tile_pool(name="picked", bufs=2))
-        plane_pool = ctx.enter_context(tc.tile_pool(name="planes", bufs=6))
+        plane_pool = ctx.enter_context(tc.tile_pool(name="planes", bufs=3))
         result_pool = ctx.enter_context(tc.tile_pool(name="result", bufs=6))
         psum_bank = ctx.enter_context(tc.psum_pool(name="psum_bank", bufs=7))
         psum_receiver = ctx.enter_context(tc.psum_pool(name="psum_receiver", bufs=1))
 
-        offsets = held.tile([P, N // 16], U16, name="offsets")
-        nc.sync.dma_start(offsets[:], offs)
         src_w = held.tile([P, BLOCKS], F32, name="src_w")
         dst_w = held.tile([P, BLOCKS], F32, name="dst_w")
         with nc.allow_non_contiguous_dma(reason="256 floats, one to a partition and block"):
-            nc.scalar.dma_start(src_w[:], p_src.rearrange("(b c) o -> c (b o)", b=BLOCKS))
+            nc.sync.dma_start(src_w[:], p_src.rearrange("(b c) o -> c (b o)", b=BLOCKS))
             nc.scalar.dma_start(dst_w[:], p_dst.rearrange("(b c) o -> c (b o)", b=BLOCKS))
         table = [held.tile([P, S], F32, name=f"table{b}") for b in range(BLOCKS)]
         for n0 in range(0, S, BANK):
             nc.sync.dma_start(table[0][:, n0 : n0 + BANK], x[0:P, n0 : n0 + BANK])
             nc.scalar.dma_start(table[1][:, n0 : n0 + BANK], x[P : 2 * P, n0 : n0 + BANK])
+        offsets = held.tile([P, N // 16], U16, name="offsets")
+        nc.sync.dma_start(offsets[:], offs)
 
         identity = held.tile([P, P], F32, name="identity")
         make_identity(nc, identity[:])
@@ -67,8 +69,7 @@ def tile_signed_gat_kernel(tc, x, p_dst, p_src, offs, out):
         def round_part(n0):
             nodes = slice(n0, n0 + BANK)
             nc.vector.tensor_copy(x_bf[0][:, nodes], table[0][:, nodes])
-            second = nc.vector if n0 == S - BANK else nc.gpsimd
-            second.tensor_copy(x_bf[1][:, nodes], table[1][:, nodes])
+            nc.vector.tensor_copy(x_bf[1][:, nodes], table[1][:, nodes])
 
         def sum_over_c(total, spread, n0):
             for b in range(BLOCKS):
@@ -100,10 +101,14 @@ def tile_signed_gat_kernel(tc, x, p_dst, p_src, offs, out):
             neighbours(n0)
             receivers(n0)
 
-        parked_scores = out[0:UNITS, 0:UNIT]
-        parked_weights = [out[s * C + UNITS : s * C + 2 * UNITS, 0:UNIT] for s in range(SIGNS)]
+        def parked_scores(units):
+            return out[SCORE_ROW[units.start] : SCORE_ROW[units.start] + len(units), 0:UNIT]
 
-        def look_up_scores(units, tag, parks, queue):
+        def parked_weights(units, s):
+            rows = out[WEIGHT_ROW0 + ROWS_OF_UNIT * units.start : WEIGHT_ROW0 + ROWS_OF_UNIT * units.stop, 0:UNIT]
+            return rows.rearrange("(u r) e -> r u e", r=ROWS_OF_UNIT)[s]
+
+        def look_up_scores(units, tag):
             scores = score_pool.tile([P, len(units) * UNIT], F32, name=tag)
             for first in range(units.start * UNIT, units.stop * UNIT, STEP):
                 j0 = first - units.start * UNIT
@@ -113,12 +118,13 @@ def tile_signed_gat_kernel(tc, x, p_dst, p_src, offs, out):
                     as_receiver[:, first // K : (first + STEP) // K, :].rearrange("c i t -> c (i t)"),
                     ALU.add,
                 )
-            for run in parks:
-                j0 = (run.start - units.start) * UNIT
-                queue.dma_start(
-                    parked_scores[run.start : run.stop, :].unsqueeze(0),
-                    scores[0:1, j0 : j0 + len(run) * UNIT].rearrange("o (u e) -> o u e", e=UNIT),
-                )
+            return scores
+
+        def park(scores, units):
+            nc.sync.dma_start(
+                parked_scores(units).unsqueeze(0),
+                scores[0:1, 0 : len(units) * UNIT].rearrange("o (u e) -> o u e", e=UNIT),
+            )
 
         def attention_weights(piece, e_tag, denom_tag):
             units = len(piece)
@@ -127,7 +133,7 @@ def tile_signed_gat_kernel(tc, x, p_dst, p_src, offs, out):
             v, e = v_and_e[:, 0], v_and_e[:, 1]
             nc.sync.dma_start(
                 v.rearrange("p (u q) t -> p u (q t)", q=NQ),
-                parked_scores[piece.start : piece.stop, :].rearrange("u (p f) -> p u f", f=PER),
+                parked_scores(piece).rearrange("u (p f) -> p u f", f=PER),
             )
             nc.vector.scalar_tensor_tensor(e, in0=v, scalar=SLOPE, in1=v, op0=ALU.mult, op1=ALU.max)
             ahead = small.tile([P, nq, K, K], F32, name="ahead")
@@ -148,7 +154,7 @@ def tile_signed_gat_kernel(tc, x, p_dst, p_src, offs, out):
             nc.vector.reciprocal(att[:], denom[:])
             for s in range(SIGNS):
                 nc.sync.dma_start(
-                    parked_weights[s][piece.start : piece.stop, :].rearrange("u (p f) -> p u f", f=PER),
+                    parked_weights(piece, s).rearrange("u (p f) -> p u f", f=PER),
                     att[:, s].rearrange("p (u q) t -> p u (q t)", q=NQ),
                 )
             wides = []
@@ -156,7 +162,7 @@ def tile_signed_gat_kernel(tc, x, p_dst, p_src, offs, out):
                 wide = score_pool.tile([P, SIGNS, UNIT], F32, name=f"wide{unit}")
                 for s in range(SIGNS):
                     nc.sync.dma_start(
-                        wide[:, s, :], parked_weights[s][unit : unit + 1, :].to_broadcast([P, UNIT])
+                        wide[:, s, :], parked_weights(range(unit, unit + 1), s).to_broadcast([P, UNIT])
                     )
                 wides.append(wide)
             return wides
@@ -185,12 +191,14 @@ def tile_signed_gat_kernel(tc, x, p_dst, p_src, offs, out):
                     )
                 nc.scalar.activation(result, total[:], ACT.Copy)
 
-        look_up_scores(range(0, 4), "scores_0_to_3", parks=(PIECES[0], PIECES[1]), queue=nc.sync)
+        early = look_up_scores(range(0, 4), "scores_0_to_3")
+        park(early, PIECES[0])
         weights = attention_weights(PIECES[0], "scores_4", "scores_5_to_6")
-        look_up_scores(range(4, 5), "scores_4", parks=(range(4, 5),), queue=nc.sync)
-        look_up_scores(range(5, 7), "scores_5_to_6", parks=(range(5, 7),), queue=nc.gpsimd)
+        park(early, range(0, 4))
+        park(look_up_scores(range(4, 5), "scores_4"), range(4, 5))
+        park(look_up_scores(range(5, 7), "scores_5_to_6"), range(5, 7))
         weights += attention_weights(PIECES[1], "scores_7", "denom_1")
-        look_up_scores(range(7, 8), "scores_7", parks=(range(7, 8),), queue=nc.gpsimd)
+        park(look_up_scores(range(7, 8), "scores_7"), range(7, 8))
         weights += attention_weights(PIECES[2], "e_2", "denom_2")
 
         for unit, wide in enumerate(weights):

@@ -25,6 +25,7 @@ STEP = UNIT // 2
 UNITS = N // UNIT
 PIECES = (range(0, 1), range(1, UNITS // 2), range(UNITS // 2, UNITS))
 
+PARK_COL = S - UNIT
 WEIGHT_ROW0, ROWS_OF_UNIT = UNITS, 3
 SCORE_ROW = [unit if unit < 4 else unit - 5 + WEIGHT_ROW0 for unit in range(UNITS)]
 
@@ -38,7 +39,7 @@ def tile_signed_gat_kernel(tc, x, p_dst, p_src, offs, out):
         score_pool = ctx.enter_context(tc.tile_pool(name="score", bufs=1))
         small = ctx.enter_context(tc.tile_pool(name="small", bufs=len(PIECES)))
         picked_pool = ctx.enter_context(tc.tile_pool(name="picked", bufs=2))
-        plane_pool = ctx.enter_context(tc.tile_pool(name="planes", bufs=3))
+        plane_pool = ctx.enter_context(tc.tile_pool(name="planes", bufs=4))
         result_pool = ctx.enter_context(tc.tile_pool(name="result", bufs=6))
         psum_bank = ctx.enter_context(tc.psum_pool(name="psum_bank", bufs=7))
         psum_receiver = ctx.enter_context(tc.psum_pool(name="psum_receiver", bufs=1))
@@ -102,10 +103,10 @@ def tile_signed_gat_kernel(tc, x, p_dst, p_src, offs, out):
             receivers(n0)
 
         def parked_scores(units):
-            return out[SCORE_ROW[units.start] : SCORE_ROW[units.start] + len(units), 0:UNIT]
+            return out[SCORE_ROW[units.start] : SCORE_ROW[units.start] + len(units), PARK_COL:]
 
         def parked_weights(units, s):
-            rows = out[WEIGHT_ROW0 + ROWS_OF_UNIT * units.start : WEIGHT_ROW0 + ROWS_OF_UNIT * units.stop, 0:UNIT]
+            rows = out[WEIGHT_ROW0 + ROWS_OF_UNIT * units.start : WEIGHT_ROW0 + ROWS_OF_UNIT * units.stop, PARK_COL:]
             return rows.rearrange("(u r) e -> r u e", r=ROWS_OF_UNIT)[s]
 
         def look_up_scores(units, tag):
@@ -199,7 +200,7 @@ def tile_signed_gat_kernel(tc, x, p_dst, p_src, offs, out):
         park(look_up_scores(range(5, 7), "scores_5_to_6"), range(5, 7))
         weights += attention_weights(PIECES[1], "scores_7", "denom_1")
         park(look_up_scores(range(7, 8), "scores_7"), range(7, 8))
-        weights += attention_weights(PIECES[2], "e_2", "denom_2")
+        weights += attention_weights(PIECES[2], "e_2", "wide1")
 
         for unit, wide in enumerate(weights):
             for s in range(SIGNS):
@@ -208,4 +209,4 @@ def tile_signed_gat_kernel(tc, x, p_dst, p_src, offs, out):
                     is_last = unit == UNITS - 1 and s == SIGNS - 1 and b == BLOCKS - 1
                     weighted_sum(results[:, b, :], wide[:, s, :], unit, b, is_last)
                 stored = out[s * C : (s + 1) * C, unit * NODES : (unit + 1) * NODES]
-                nc.sync.dma_start(stored.rearrange("(b c) i -> c b i", b=BLOCKS), results[:])
+                nc.scalar.dma_start(stored.rearrange("(b c) i -> c b i", b=BLOCKS), results[:])

@@ -21,7 +21,7 @@ UNIT = 1024
 NODES = UNIT // K
 PER = UNIT // P
 NQ = PER // K
-STEP = UNIT // 2
+PARTS = [(n0, BANK) for n0 in range(0, S - BANK, BANK)] + [(n0, BANK // 2) for n0 in range(S - BANK, S, BANK // 2)]
 UNITS = N // UNIT
 PIECES = (range(0, 1), range(1, UNITS // 2), range(UNITS // 2, UNITS))
 
@@ -50,9 +50,9 @@ def tile_signed_gat_kernel(tc, x, p_dst, p_src, offs, out):
             nc.sync.dma_start(src_w[:], p_src.rearrange("(b c) o -> c (b o)", b=BLOCKS))
             nc.scalar.dma_start(dst_w[:], p_dst.rearrange("(b c) o -> c (b o)", b=BLOCKS))
         table = [held.tile([P, S], F32, name=f"table{b}") for b in range(BLOCKS)]
-        for n0 in range(0, S, BANK):
-            nc.sync.dma_start(table[0][:, n0 : n0 + BANK], x[0:P, n0 : n0 + BANK])
-            nc.scalar.dma_start(table[1][:, n0 : n0 + BANK], x[P : 2 * P, n0 : n0 + BANK])
+        for n0, width in PARTS:
+            nc.sync.dma_start(table[0][:, n0 : n0 + width], x[0:P, n0 : n0 + width])
+            nc.scalar.dma_start(table[1][:, n0 : n0 + width], x[P : 2 * P, n0 : n0 + width])
         offsets = held.tile([P, N // 16], U16, name="offsets")
         nc.sync.dma_start(offsets[:], offs)
 
@@ -67,39 +67,40 @@ def tile_signed_gat_kernel(tc, x, p_dst, p_src, offs, out):
         as_neighbour = held.tile([P, S], F32, name="as_neighbour")
         as_receiver = held.tile([P, S, K], F32, name="as_receiver")
 
-        def round_part(n0):
-            nodes = slice(n0, n0 + BANK)
+        def round_part(n0, width):
+            nodes = slice(n0, n0 + width)
             nc.vector.tensor_copy(x_bf[0][:, nodes], table[0][:, nodes])
             nc.vector.tensor_copy(x_bf[1][:, nodes], table[1][:, nodes])
 
-        def sum_over_c(total, spread, n0):
+        def sum_over_c(total, spread, n0, width):
             for b in range(BLOCKS):
                 nc.tensor.matmul(
                     total[:],
                     lhsT=spread[:, b, :],
-                    rhs=x_bf[b][:, n0 : n0 + BANK],
+                    rhs=x_bf[b][:, n0 : n0 + width],
                     start=(b == 0),
                     stop=(b == BLOCKS - 1),
                 )
 
-        def neighbours(n0):
-            src_sum = psum_bank.tile([P, BANK], F32, name="bank")
-            sum_over_c(src_sum, src_spread, n0)
-            nc.vector.tensor_copy(as_neighbour[:, n0 : n0 + BANK], src_sum[:])
+        def neighbours(n0, width):
+            src_sum = psum_bank.tile([P, width], F32, name="bank")
+            sum_over_c(src_sum, src_spread, n0, width)
+            nc.vector.tensor_copy(as_neighbour[:, n0 : n0 + width], src_sum[:])
 
         def receivers(n0):
             dst_sum = psum_receiver.tile([P, BANK], F32, name="receiver")
-            sum_over_c(dst_sum, dst_spread, n0)
-            for i0 in range(0, BANK, STEP // K):
+            sum_over_c(dst_sum, dst_spread, n0, BANK)
+            for i0 in range(0, BANK, NODES):
                 nc.scalar.activation(
-                    as_receiver[:, n0 + i0 : n0 + i0 + STEP // K, :],
-                    dst_sum[:, i0 : i0 + STEP // K].unsqueeze(2).to_broadcast([P, STEP // K, K]),
+                    as_receiver[:, n0 + i0 : n0 + i0 + NODES, :],
+                    dst_sum[:, i0 : i0 + NODES].unsqueeze(2).to_broadcast([P, NODES, K]),
                     ACT.Copy,
                 )
 
+        for n0, width in PARTS:
+            round_part(n0, width)
+            neighbours(n0, width)
         for n0 in range(0, S, BANK):
-            round_part(n0)
-            neighbours(n0)
             receivers(n0)
 
         def parked_scores(units):
@@ -111,12 +112,12 @@ def tile_signed_gat_kernel(tc, x, p_dst, p_src, offs, out):
 
         def look_up_scores(units, tag):
             scores = score_pool.tile([P, len(units) * UNIT], F32, name=tag)
-            for first in range(units.start * UNIT, units.stop * UNIT, STEP):
-                j0 = first - units.start * UNIT
+            for unit in units:
+                j0 = (unit - units.start) * UNIT
                 nc.vector.tensor_tensor(
-                    scores[:, j0 : j0 + STEP],
-                    as_neighbour[:].indirect(offsets[:, first // 16 : (first + STEP) // 16]),
-                    as_receiver[:, first // K : (first + STEP) // K, :].rearrange("c i t -> c (i t)"),
+                    scores[:, j0 : j0 + UNIT],
+                    as_neighbour[:].indirect(offsets[:, unit * UNIT // 16 : (unit + 1) * UNIT // 16]),
+                    as_receiver[:, unit * NODES : (unit + 1) * NODES, :].rearrange("c i t -> c (i t)"),
                     ALU.add,
                 )
             return scores
@@ -209,4 +210,4 @@ def tile_signed_gat_kernel(tc, x, p_dst, p_src, offs, out):
                     is_last = unit == UNITS - 1 and s == SIGNS - 1 and b == BLOCKS - 1
                     weighted_sum(results[:, b, :], wide[:, s, :], unit, b, is_last)
                 stored = out[s * C : (s + 1) * C, unit * NODES : (unit + 1) * NODES]
-                nc.scalar.dma_start(stored.rearrange("(b c) i -> c b i", b=BLOCKS), results[:])
+                nc.sync.dma_start(stored.rearrange("(b c) i -> c b i", b=BLOCKS), results[:])

@@ -103,29 +103,30 @@ def tile_signed_gat_kernel(tc, x, p_dst, p_src, offs, out):
         for n0 in range(0, S, BANK):
             receivers(n0)
 
-        def parked_scores(units):
-            return out[SCORE_ROW[units.start] : SCORE_ROW[units.start] + len(units), PARK_COL:]
-
         def parked_weights(units, s):
             rows = out[WEIGHT_ROW0 + ROWS_OF_UNIT * units.start : WEIGHT_ROW0 + ROWS_OF_UNIT * units.stop, PARK_COL:]
             return rows.rearrange("(u r) e -> r u e", r=ROWS_OF_UNIT)[s]
 
-        def look_up_scores(units, tag):
-            scores = score_pool.tile([P, len(units) * UNIT], F32, name=tag)
-            for unit in units:
-                j0 = (unit - units.start) * UNIT
-                nc.vector.tensor_tensor(
-                    scores[:, j0 : j0 + UNIT],
-                    as_neighbour[:].indirect(offsets[:, unit * UNIT // 16 : (unit + 1) * UNIT // 16]),
-                    as_receiver[:, unit * NODES : (unit + 1) * NODES, :].rearrange("c i t -> c (i t)"),
-                    ALU.add,
-                )
+        def look_up_scores(first, end, tag):
+            scores = score_pool.tile([P, end - first], F32, name=tag)
+            for unit in range(first // UNIT, end // UNIT + 1):
+                j0, j1 = max(first, unit * UNIT), min(end, (unit + 1) * UNIT)
+                if j0 < j1:
+                    nc.vector.tensor_tensor(
+                        scores[:, j0 - first : j1 - first],
+                        as_neighbour[:].indirect(offsets[:, j0 // 16 : j1 // 16]),
+                        as_receiver[:, j0 // K : j1 // K, :].rearrange("c i t -> c (i t)"),
+                        ALU.add,
+                    )
             return scores
 
-        def park(scores, units):
+        def park(scores, first):
+            size = scores.shape[1]
+            width = min(size, UNIT)
+            row, col = SCORE_ROW[first // UNIT], PARK_COL + first % UNIT
             nc.sync.dma_start(
-                parked_scores(units).unsqueeze(0),
-                scores[0:1, 0 : len(units) * UNIT].rearrange("o (u e) -> o u e", e=UNIT),
+                out[row : row + size // width, col : col + width].unsqueeze(0),
+                scores[0:1, :].rearrange("o (u e) -> o u e", e=width),
             )
 
         def attention_weights(piece, e_tag, denom_tag):
@@ -135,7 +136,9 @@ def tile_signed_gat_kernel(tc, x, p_dst, p_src, offs, out):
             v, e = v_and_e[:, 0], v_and_e[:, 1]
             nc.sync.dma_start(
                 v.rearrange("p (u q) t -> p u (q t)", q=NQ),
-                parked_scores(piece).rearrange("u (p f) -> p u f", f=PER),
+                out[SCORE_ROW[piece.start] : SCORE_ROW[piece.start] + units, PARK_COL:].rearrange(
+                    "u (p f) -> p u f", f=PER
+                ),
             )
             nc.vector.scalar_tensor_tensor(e, in0=v, scalar=SLOPE, in1=v, op0=ALU.mult, op1=ALU.max)
             ahead = small.tile([P, nq, K, K], F32, name="ahead")
@@ -169,45 +172,51 @@ def tile_signed_gat_kernel(tc, x, p_dst, p_src, offs, out):
                 wides.append(wide)
             return wides
 
-        def weighted_sum(result, a, unit, b, is_last):
-            picked = picked_pool.tile([P, UNIT], F32, name="picked")
+        def weighted_sum(result, a, first, end, b, by_vector):
+            nodes = (end - first) // K
+            picked = picked_pool.tile([P, end - first], F32, name="picked")
             nc.vector.tensor_tensor(
-                picked[:],
-                table[b][:].indirect(offsets[:, unit * UNIT // 16 : (unit + 1) * UNIT // 16]),
-                a,
-                ALU.mult,
+                picked[:], table[b][:].indirect(offsets[:, first // 16 : end // 16]), a, ALU.mult
             )
-            if is_last:
+            if by_vector:
                 nc.vector.tensor_reduce(
                     result, picked[:].rearrange("c (i t) -> c i t", t=K), axis=AXIS.X, op=ALU.add
                 )
             else:
-                planes = plane_pool.tile([P, K, NODES], F32, name="planes")
+                planes = plane_pool.tile([P, K, nodes], F32, name="planes")
                 nc.scalar.activation(
                     planes[:].rearrange("c t i -> c i t"), picked[:].rearrange("c (i t) -> c i t", t=K), ACT.Copy
                 )
-                total = psum_bank.tile([P, NODES], F32, name="bank")
+                total = psum_bank.tile([P, nodes], F32, name="bank")
                 for t in range(K):
                     nc.tensor.matmul(
                         total[:], lhsT=identity[:], rhs=planes[:, t, :], start=(t == 0), stop=(t == K - 1)
                     )
                 nc.scalar.activation(result, total[:], ACT.Copy)
 
-        early = look_up_scores(range(0, 4), "scores_0_to_3")
-        park(early, PIECES[0])
-        weights = attention_weights(PIECES[0], "scores_4", "scores_5_to_6")
-        park(early, range(0, 4))
-        park(look_up_scores(range(4, 5), "scores_4"), range(4, 5))
-        park(look_up_scores(range(5, 7), "scores_5_to_6"), range(5, 7))
+        early = look_up_scores(0, 4 * UNIT, "scores_0_to_3")
+        park(early[:, 0:UNIT], 0)
+        weights = attention_weights(PIECES[0], "scores_4a", "scores_4b_to_6")
+        park(early[:], 0)
+        half = 4 * UNIT + UNIT // 2
+        park(look_up_scores(4 * UNIT, half, "scores_4a")[:], 4 * UNIT)
+        later = look_up_scores(half, 7 * UNIT, "scores_4b_to_6")
+        park(later[:, 0 : UNIT // 2], half)
+        park(later[:, UNIT // 2 :], 5 * UNIT)
         weights += attention_weights(PIECES[1], "scores_7", "denom_1")
-        park(look_up_scores(range(7, 8), "scores_7"), range(7, 8))
+        park(look_up_scores(7 * UNIT, N, "scores_7")[:], 7 * UNIT)
         weights += attention_weights(PIECES[2], "e_2", "wide1")
 
         for unit, wide in enumerate(weights):
             for s in range(SIGNS):
                 results = result_pool.tile([P, BLOCKS, NODES], F32, name="results")
+                last = unit == UNITS - 1 and s == SIGNS - 1
                 for b in range(BLOCKS):
-                    is_last = unit == UNITS - 1 and s == SIGNS - 1 and b == BLOCKS - 1
-                    weighted_sum(results[:, b, :], wide[:, s, :], unit, b, is_last)
+                    by_vector = last and b == BLOCKS - 1
+                    parts = 2 if last and not by_vector else 1
+                    for j0 in range(0, UNIT, UNIT // parts):
+                        j1 = j0 + UNIT // parts
+                        first, end = unit * UNIT + j0, unit * UNIT + j1
+                        weighted_sum(results[:, b, j0 // K : j1 // K], wide[:, s, j0:j1], first, end, b, by_vector)
                 stored = out[s * C : (s + 1) * C, unit * NODES : (unit + 1) * NODES]
                 nc.sync.dma_start(stored.rearrange("(b c) i -> c b i", b=BLOCKS), results[:])

@@ -38,8 +38,8 @@ def tile_signed_gat_kernel(tc, x, p_dst, p_src, offs, out):
         held = ctx.enter_context(tc.tile_pool(name="held", bufs=1))
         score_pool = ctx.enter_context(tc.tile_pool(name="score", bufs=1))
         small = ctx.enter_context(tc.tile_pool(name="small", bufs=len(PIECES)))
-        picked_pool = ctx.enter_context(tc.tile_pool(name="picked", bufs=2))
-        plane_pool = ctx.enter_context(tc.tile_pool(name="planes", bufs=4))
+        picked_pool = ctx.enter_context(tc.tile_pool(name="picked", bufs=3))
+        plane_pool = ctx.enter_context(tc.tile_pool(name="planes", bufs=3))
         result_pool = ctx.enter_context(tc.tile_pool(name="result", bufs=6))
         psum_bank = ctx.enter_context(tc.psum_pool(name="psum_bank", bufs=7))
         psum_receiver = ctx.enter_context(tc.psum_pool(name="psum_receiver", bufs=1))
@@ -85,7 +85,10 @@ def tile_signed_gat_kernel(tc, x, p_dst, p_src, offs, out):
         def neighbours(n0, width):
             src_sum = psum_bank.tile([P, width], F32, name="bank")
             sum_over_c(src_sum, src_spread, n0, width)
-            nc.vector.tensor_copy(as_neighbour[:, n0 : n0 + width], src_sum[:])
+            if n0 < S - BANK:
+                nc.scalar.activation(as_neighbour[:, n0 : n0 + width], src_sum[:], ACT.Copy)
+            else:
+                nc.vector.tensor_copy(as_neighbour[:, n0 : n0 + width], src_sum[:])
 
         def receivers(n0):
             dst_sum = psum_receiver.tile([P, BANK], F32, name="receiver")

@@ -106,30 +106,29 @@ def tile_signed_gat_kernel(tc, x, p_dst, p_src, offs, out):
         for n0 in range(0, S, BANK):
             receivers(n0)
 
+        def parked_scores(units):
+            return out[SCORE_ROW[units.start] : SCORE_ROW[units.start] + len(units), PARK_COL:]
+
         def parked_weights(units, s):
             rows = out[WEIGHT_ROW0 + ROWS_OF_UNIT * units.start : WEIGHT_ROW0 + ROWS_OF_UNIT * units.stop, PARK_COL:]
             return rows.rearrange("(u r) e -> r u e", r=ROWS_OF_UNIT)[s]
 
-        def look_up_scores(first, end, tag):
-            scores = score_pool.tile([P, end - first], F32, name=tag)
-            for unit in range(first // UNIT, end // UNIT + 1):
-                j0, j1 = max(first, unit * UNIT), min(end, (unit + 1) * UNIT)
-                if j0 < j1:
-                    nc.vector.tensor_tensor(
-                        scores[:, j0 - first : j1 - first],
-                        as_neighbour[:].indirect(offsets[:, j0 // 16 : j1 // 16]),
-                        as_receiver[:, j0 // K : j1 // K, :].rearrange("c i t -> c (i t)"),
-                        ALU.add,
-                    )
+        def look_up_scores(units, tag):
+            scores = score_pool.tile([P, len(units) * UNIT], F32, name=tag)
+            for unit in units:
+                j0 = (unit - units.start) * UNIT
+                nc.vector.tensor_tensor(
+                    scores[:, j0 : j0 + UNIT],
+                    as_neighbour[:].indirect(offsets[:, unit * UNIT // 16 : (unit + 1) * UNIT // 16]),
+                    as_receiver[:, unit * NODES : (unit + 1) * NODES, :].rearrange("c i t -> c (i t)"),
+                    ALU.add,
+                )
             return scores
 
-        def park(scores, first):
-            size = scores.shape[1]
-            width = min(size, UNIT)
-            row, col = SCORE_ROW[first // UNIT], PARK_COL + first % UNIT
+        def park(scores, units):
             nc.sync.dma_start(
-                out[row : row + size // width, col : col + width].unsqueeze(0),
-                scores[0:1, :].rearrange("o (u e) -> o u e", e=width),
+                parked_scores(units).unsqueeze(0),
+                scores[0:1, 0 : len(units) * UNIT].rearrange("o (u e) -> o u e", e=UNIT),
             )
 
         def attention_weights(piece, e_tag, denom_tag):
@@ -139,9 +138,7 @@ def tile_signed_gat_kernel(tc, x, p_dst, p_src, offs, out):
             v, e = v_and_e[:, 0], v_and_e[:, 1]
             nc.sync.dma_start(
                 v.rearrange("p (u q) t -> p u (q t)", q=NQ),
-                out[SCORE_ROW[piece.start] : SCORE_ROW[piece.start] + units, PARK_COL:].rearrange(
-                    "u (p f) -> p u f", f=PER
-                ),
+                parked_scores(piece).rearrange("u (p f) -> p u f", f=PER),
             )
             nc.vector.scalar_tensor_tensor(e, in0=v, scalar=SLOPE, in1=v, op0=ALU.mult, op1=ALU.max)
             ahead = small.tile([P, nq, K, K], F32, name="ahead")
@@ -197,17 +194,14 @@ def tile_signed_gat_kernel(tc, x, p_dst, p_src, offs, out):
                     )
                 nc.scalar.activation(result, total[:], ACT.Copy)
 
-        early = look_up_scores(0, 4 * UNIT, "scores_0_to_3")
-        park(early[:, 0:UNIT], 0)
-        weights = attention_weights(PIECES[0], "scores_4a", "scores_4b_to_6")
-        park(early[:], 0)
-        half = 4 * UNIT + UNIT // 2
-        park(look_up_scores(4 * UNIT, half, "scores_4a")[:], 4 * UNIT)
-        later = look_up_scores(half, 7 * UNIT, "scores_4b_to_6")
-        park(later[:, 0 : UNIT // 2], half)
-        park(later[:, UNIT // 2 :], 5 * UNIT)
+        early = look_up_scores(range(0, 4), "scores_0_to_3")
+        park(early, PIECES[0])
+        weights = attention_weights(PIECES[0], "scores_4", "scores_5_to_6")
+        park(early, range(0, 4))
+        park(look_up_scores(range(4, 5), "scores_4"), range(4, 5))
+        park(look_up_scores(range(5, 7), "scores_5_to_6"), range(5, 7))
         weights += attention_weights(PIECES[1], "scores_7", "denom_1")
-        park(look_up_scores(7 * UNIT, N, "scores_7")[:], 7 * UNIT)
+        park(look_up_scores(range(7, 8), "scores_7"), range(7, 8))
         weights += attention_weights(PIECES[2], "e_2", "wide1")
 
         for unit, wide in enumerate(weights):

from contextlib import ExitStack

import concourse.mybir as mybir
from concourse.masks import make_identity

F32 = mybir.dt.float32
BF16 = mybir.dt.bfloat16
U16 = mybir.dt.uint16
ALU = mybir.AluOpType
ACT = mybir.ActivationFunctionType
AXIS = mybir.AxisListType

P = 128
C, S, K, N = 256, 2048, 4, 8192
BLOCKS = C // P
SLOPE = 0.3
SIGNS = 2
BANK = 512

UNIT = 1024
NODES = UNIT // K
PER = UNIT // P
NQ = PER // K
PARTS = [(n0, BANK) for n0 in range(0, S - BANK, BANK)] + [(n0, BANK // 2) for n0 in range(S - BANK, S, BANK // 2)]
UNITS = N // UNIT
PIECES = (range(0, 1), range(1, UNITS // 2), range(UNITS // 2, UNITS))

PARK_COL = S - UNIT
WEIGHT_ROW0, ROWS_OF_UNIT = UNITS, 3
SCORE_ROW = [unit if unit < 4 else unit - 5 + WEIGHT_ROW0 for unit in range(UNITS)]

FLOPS = 2 * C * N + 2 * C * S + SIGNS * 2 * C * N


def tile_signed_gat_kernel(tc, x, p_dst, p_src, offs, out):
    nc = tc.nc
    with ExitStack() as ctx:
        held = ctx.enter_context(tc.tile_pool(name="held", bufs=1))
        score_pool = ctx.enter_context(tc.tile_pool(name="score", bufs=1))
        small = ctx.enter_context(tc.tile_pool(name="small", bufs=len(PIECES)))
        picked_pool = ctx.enter_context(tc.tile_pool(name="picked", bufs=3))
        plane_pool = ctx.enter_context(tc.tile_pool(name="planes", bufs=3))
        result_pool = ctx.enter_context(tc.tile_pool(name="result", bufs=6))
        psum_bank = ctx.enter_context(tc.psum_pool(name="psum_bank", bufs=7))
        psum_receiver = ctx.enter_context(tc.psum_pool(name="psum_receiver", bufs=1))

        src_w = held.tile([P, BLOCKS], F32, name="src_w")
        dst_w = held.tile([P, BLOCKS], F32, name="dst_w")
        with nc.allow_non_contiguous_dma(reason="256 floats, one to a partition and block"):
            nc.sync.dma_start(src_w[:], p_src.rearrange("(b c) o -> c (b o)", b=BLOCKS))
            nc.scalar.dma_start(dst_w[:], p_dst.rearrange("(b c) o -> c (b o)", b=BLOCKS))
        table = [held.tile([P, S], F32, name=f"table{b}") for b in range(BLOCKS)]
        for n0, width in PARTS:
            nc.sync.dma_start(table[0][:, n0 : n0 + width], x[0:P, n0 : n0 + width])
            nc.scalar.dma_start(table[1][:, n0 : n0 + width], x[P : 2 * P, n0 : n0 + width])
        offsets = held.tile([P, N // 16], U16, name="offsets")
        nc.sync.dma_start(offsets[:], offs)

        identity = held.tile([P, P], F32, name="identity")
        make_identity(nc, identity[:])
        src_spread = held.tile([P, BLOCKS, P], BF16, name="src_spread")
        nc.vector.tensor_copy(src_spread[:], src_w[:].unsqueeze(2).to_broadcast([P, BLOCKS, P]))
        dst_spread = held.tile([P, BLOCKS, P], BF16, name="dst_spread")
        nc.vector.tensor_copy(dst_spread[:], dst_w[:].unsqueeze(2).to_broadcast([P, BLOCKS, P]))

        x_bf = [held.tile([P, S], BF16, name=f"x_bf{b}") for b in range(BLOCKS)]
        as_neighbour = held.tile([P, S], F32, name="as_neighbour")
        as_receiver = held.tile([P, S, K], F32, name="as_receiver")

        def round_part(n0, width):
            nodes = slice(n0, n0 + width)
            nc.vector.tensor_copy(x_bf[0][:, nodes], table[0][:, nodes])
            nc.vector.tensor_copy(x_bf[1][:, nodes], table[1][:, nodes])

        def sum_over_c(total, spread, n0, width):
            for b in range(BLOCKS):
                nc.tensor.matmul(
                    total[:],
                    lhsT=spread[:, b, :],
                    rhs=x_bf[b][:, n0 : n0 + width],
                    start=(b == 0),
                    stop=(b == BLOCKS - 1),
                )

        def neighbours(n0, width):
            src_sum = psum_bank.tile([P, width], F32, name="bank")
            sum_over_c(src_sum, src_spread, n0, width)
            if n0 < S - BANK:
                nc.scalar.activation(as_neighbour[:, n0 : n0 + width], src_sum[:], ACT.Copy)
            else:
                nc.vector.tensor_copy(as_neighbour[:, n0 : n0 + width], src_sum[:])

        def receivers(n0):
            dst_sum = psum_receiver.tile([P, BANK], F32, name="receiver")
            sum_over_c(dst_sum, dst_spread, n0, BANK)
            for i0 in range(0, BANK, NODES):
                nc.scalar.activation(
                    as_receiver[:, n0 + i0 : n0 + i0 + NODES, :],
                    dst_sum[:, i0 : i0 + NODES].unsqueeze(2).to_broadcast([P, NODES, K]),
                    ACT.Copy,
                )

        for n0, width in PARTS:
            round_part(n0, width)
            neighbours(n0, width)
        for n0 in range(0, S, BANK):
            receivers(n0)

        def parked_scores(units):
            return out[SCORE_ROW[units.start] : SCORE_ROW[units.start] + len(units), PARK_COL:]

        def parked_weights(units, s):
            rows = out[WEIGHT_ROW0 + ROWS_OF_UNIT * units.start : WEIGHT_ROW0 + ROWS_OF_UNIT * units.stop, PARK_COL:]
            return rows.rearrange("(u r) e -> r u e", r=ROWS_OF_UNIT)[s]

        def look_up_scores(units, tag):
            scores = score_pool.tile([P, len(units) * UNIT], F32, name=tag)
            for unit in units:
                j0 = (unit - units.start) * UNIT
                nc.vector.tensor_tensor(
                    scores[:, j0 : j0 + UNIT],
                    as_neighbour[:].indirect(offsets[:, unit * UNIT // 16 : (unit + 1) * UNIT // 16]),
                    as_receiver[:, unit * NODES : (unit + 1) * NODES, :].rearrange("c i t -> c (i t)"),
                    ALU.add,
                )
            return scores

        def park(scores, units):
            nc.sync.dma_start(
                parked_scores(units).unsqueeze(0),
                scores[0:1, 0 : len(units) * UNIT].rearrange("o (u e) -> o u e", e=UNIT),
            )

        def attention_weights(piece, e_tag, denom_tag):
            units = len(piece)
            nq = units * NQ
            v_and_e = score_pool.tile([P, 2, nq, K], F32, name=e_tag)
            v, e = v_and_e[:, 0], v_and_e[:, 1]
            nc.sync.dma_start(
                v.rearrange("p (u q) t -> p u (q t)", q=NQ),
                parked_scores(piece).rearrange("u (p f) -> p u f", f=PER),
            )
            nc.vector.scalar_tensor_tensor(e, in0=v, scalar=SLOPE, in1=v, op0=ALU.mult, op1=ALU.max)
            ahead = small.tile([P, nq, K, K], F32, name="ahead")
            nc.vector.tensor_tensor(
                ahead[:],
                e.unsqueeze(2).to_broadcast([P, nq, K, K]),
                e.unsqueeze(3).to_broadcast([P, nq, K, K]),
                ALU.subtract,
            )
            terms = small.tile([P, nq, K, K], F32, name="terms")
            nc.scalar.activation(terms[:], ahead[:], ACT.Exp)
            denom = score_pool.tile([P, SIGNS, nq, K], F32, name=denom_tag)
            nc.vector.tensor_reduce(denom[:, 0], terms[:], axis=AXIS.X, op=ALU.add)
            nc.vector.tensor_reduce(
                denom[:, 1], terms[:].rearrange("p q t u -> p q u t"), axis=AXIS.X, op=ALU.add, negate=True
            )
            att = small.tile([P, SIGNS, nq, K], F32, name="att")
            nc.vector.reciprocal(att[:], denom[:])
            for s in range(SIGNS):
                nc.sync.dma_start(
                    parked_weights(piece, s).rearrange("u (p f) -> p u f", f=PER),
                    att[:, s].rearrange("p (u q) t -> p u (q t)", q=NQ),
                )
            wides = []
            for unit in piece:
                wide = score_pool.tile([P, SIGNS, UNIT], F32, name=f"wide{unit}")
                for s in range(SIGNS):
                    nc.sync.dma_start(
                        wide[:, s, :], parked_weights(range(unit, unit + 1), s).to_broadcast([P, UNIT])
                    )
                wides.append(wide)
            return wides

        def weighted_sum(result, a, first, end, b, by_vector):
            nodes = (end - first) // K
            picked = picked_pool.tile([P, end - first], F32, name="picked")
            nc.vector.tensor_tensor(
                picked[:], table[b][:].indirect(offsets[:, first // 16 : end // 16]), a, ALU.mult
            )
            if by_vector:
                nc.vector.tensor_reduce(
                    result, picked[:].rearrange("c (i t) -> c i t", t=K), axis=AXIS.X, op=ALU.add
                )
            else:
                planes = plane_pool.tile([P, K, nodes], F32, name="planes")
                nc.scalar.activation(
                    planes[:].rearrange("c t i -> c i t"), picked[:].rearrange("c (i t) -> c i t", t=K), ACT.Copy
                )
                total = psum_bank.tile([P, nodes], F32, name="bank")
                for t in range(K):
                    nc.tensor.matmul(
                        total[:], lhsT=identity[:], rhs=planes[:, t, :], start=(t == 0), stop=(t == K - 1)
                    )
                nc.scalar.activation(result, total[:], ACT.Copy)

        early = look_up_scores(range(0, 4), "scores_0_to_3")
        park(early, PIECES[0])
        weights = attention_weights(PIECES[0], "scores_4", "scores_5_to_6")
        park(early, range(0, 4))
        park(look_up_scores(range(4, 5), "scores_4"), range(4, 5))
        park(look_up_scores(range(5, 7), "scores_5_to_6"), range(5, 7))
        weights += attention_weights(PIECES[1], "scores_7", "denom_1")
        park(look_up_scores(range(7, 8), "scores_7"), range(7, 8))
        weights += attention_weights(PIECES[2], "e_2", "wide1")

        for unit, wide in enumerate(weights):
            for s in range(SIGNS):
                results = result_pool.tile([P, BLOCKS, NODES], F32, name="results")
                last = unit == UNITS - 1 and s == SIGNS - 1
                for b in range(BLOCKS):
                    by_vector = last and b == BLOCKS - 1
                    parts = 2 if last and not by_vector else 1
                    for j0 in range(0, UNIT, UNIT // parts):
                        j1 = j0 + UNIT // parts
                        first, end = unit * UNIT + j0, unit * UNIT + j1
                        weighted_sum(results[:, b, j0 // K : j1 // K], wide[:, s, j0:j1], first, end, b, by_vector)
                stored = out[s * C : (s + 1) * C, unit * NODES : (unit + 1) * NODES]
                nc.sync.dma_start(stored.rearrange("(b c) i -> c b i", b=BLOCKS), results[:])
